import numpy as np
import ml_dtypes


def mxq(x, axis, fmt="e4m3"):
    dtype, down = {"e4m3": (ml_dtypes.float8_e4m3fn, 7), "e5m2": (ml_dtypes.float8_e5m2, 14)}[fmt]
    v = np.moveaxis(np.asarray(x, np.float32).astype(ml_dtypes.bfloat16).astype(np.float64), axis, -1)
    blocks = v.reshape(v.shape[:-1] + (-1, 32))
    amax = np.abs(blocks).max(-1, keepdims=True)
    byte = np.maximum(np.where(amax > 0, np.frexp(amax)[1] - 1 + 127, 0) - down, 1)
    scale = np.exp2(byte - 127.0)
    codes = (blocks / scale).astype(np.float32).astype(dtype).astype(np.float64)
    return np.moveaxis((codes * scale).reshape(v.shape), -1, axis)


WIDE = False


def mx_kscale(k):
    if not WIDE:
        return np.ones(k)
    levels = np.array([10, -10, 5, -5, 0])
    a = np.random.permutation(np.resize(levels, k // 512 * 4)).reshape(k // 512, 4)
    idx = np.arange(k)
    return np.exp2(a[idx // 512, idx % 128 // 32])


BF16 = ml_dtypes.bfloat16


def bf(x):
    return np.asarray(x, np.float32).astype(BF16)


def f64(x):
    return np.asarray(x).astype(np.float64)


T, HS, WS, WT, WH, WW, NH, HD, VID_DIM, TXT_DIM, TXT_LEN = 8, 8, 16, 8, 8, 8, 8, 128, 1536, 1536, 256
L_VID = T * HS * WS
N_WIN = (T // WT) * (HS // WH) * (WS // WW)
WIN_LEN = WT * WH * WW
INNER = NH * HD


def window_reverse(x):
    x = x.reshape(T // WT, HS // WH, WS // WW, WT, WH, WW, NH, HD)
    x = x.transpose(0, 3, 1, 4, 2, 5, 6, 7)
    return x.reshape(L_VID, INNER)


def setup_inputs():
    t = mx_kscale(INNER)
    mu = np.sign(np.random.standard_normal((NH, HD))) * (0.4 + 0.2 * np.random.random((NH, HD)))
    return {
        "qw": bf(np.random.standard_normal((N_WIN, WIN_LEN, NH, HD))),
        "kw": bf(np.random.standard_normal((N_WIN, WIN_LEN, NH, HD))),
        "vw": bf((mu + np.random.standard_normal((N_WIN, WIN_LEN, NH, HD))) * t.reshape(NH, HD)),
        "Wo_vid": bf(np.random.standard_normal((INNER, VID_DIM)) * 2.0 / np.sqrt(INNER) / t[:, None]),
        "bo_vid": bf(0.1 * np.random.standard_normal(VID_DIM)),
    }


def reference(qw, kw, vw, Wo_vid, bo_vid):
    scale = 1.0 / np.sqrt(HD)
    s = f64(qw).transpose(0, 2, 1, 3) @ f64(kw).transpose(0, 2, 3, 1) * scale
    e = np.exp(s - s.max(-1, keepdims=True))
    o = (mxq(e, 3, "e4m3") @ mxq(f64(vw).transpose(0, 2, 1, 3), 2, "e4m3")) / e.sum(-1, keepdims=True)
    o = window_reverse(o.transpose(0, 2, 1, 3))
    return (mxq(o, 1, "e4m3") @ mxq(f64(Wo_vid), 0, "e4m3")) + f64(bo_vid)

@@ -1,0 +1,299 @@
+from contextlib import ExitStack
+
+import concourse.mybir as mybir
+from concourse.masks import make_identity
+
+BF16 = mybir.dt.bfloat16
+F32 = mybir.dt.float32
+U32 = mybir.dt.uint32
+U8 = mybir.dt.uint8
+FP8X4 = mybir.dt.float8_e4m3fn_x4
+ALU = mybir.AluOpType
+ACT = mybir.ActivationFunctionType
+
+P = 128
+N_WIN = 2
+WIN_LEN = 512
+NH = 8
+HD = 128
+INNER = NH * HD
+VID_DIM = 1536
+Q_TILES = WIN_LEN // P
+N_TILES = N_WIN * Q_TILES
+N_STEPS = N_TILES * NH
+K_PASS = 512
+F_PASSES = INNER // K_PASS
+BANK = 512
+OUT_BANKS = VID_DIM // BANK
+SCALE = 1.0 / (HD ** 0.5)
+
+FLOPS = 2 * 2 * N_WIN * NH * WIN_LEN * WIN_LEN * HD + 2 * N_WIN * WIN_LEN * INNER * VID_DIM
+
+PREP_LEAD = 2
+FLIP_LAG = 4
+RECIP_LAG = 5
+QUANT_LAG = 8
+ATTEND_LAG = 9
+XFLIP_LAG = 10
+XQUANT_LAG = 14
+PROJECT_LAG = 15
+
+
+def tile_naswinattention_pb_kernel(tc, qw, kw, vw, Wo_vid, bo_vid, out):
+    nc = tc.nc
+    with ExitStack() as ctx:
+        keep = ctx.enter_context(tc.tile_pool(name="keep", bufs=1))
+        work = ctx.enter_context(tc.tile_pool(name="work", bufs=2))
+        s_banks = ctx.enter_context(tc.psum_pool(name="s_banks", bufs=4))
+        aux_banks = ctx.enter_context(tc.psum_pool(name="aux_banks", bufs=4))
+        ctx.enter_context(tc.manual_schedule())
+
+        ident_bf = keep.tile([P, P], BF16, name="ident_bf")
+        make_identity(nc, ident_bf[:])
+        ident_f32 = keep.tile([P, P], F32, name="ident_f32")
+        make_identity(nc, ident_f32[:])
+
+        q_raw = [keep.tile([P, Q_TILES, INNER], BF16, name="q_raw%d" % n) for n in range(N_WIN)]
+        k_raw = [keep.tile([P, Q_TILES, INNER], BF16, name="k_raw%d" % n) for n in range(N_WIN)]
+        v_raw = [keep.tile([P, 2, 2 * INNER], BF16, name="v_raw%d" % n) for n in range(N_WIN)]
+        wo_raw = keep.tile([P, 2 * F_PASSES, 2 * VID_DIM], BF16, name="wo_raw")
+        bias_bc = keep.tile([P, VID_DIM], BF16, name="bias_bc")
+
+        def load_tokens(dst, src, n, tiles):
+            view = src[n].rearrange("(t p) g d -> p t (g d)", p=P)
+            for t in tiles:
+                nc.sync.dma_start(out=dst[n][:, t, :], in_=view[:, t, :])
+
+        def load_values(n):
+            nc.sync.dma_start(
+                out=v_raw[n][:], in_=vw[n].rearrange("(u p e) g d -> p u (e g d)", u=2, e=2)
+            )
+
+        load_tokens(q_raw, qw, 0, [0])
+        load_tokens(k_raw, kw, 0, range(Q_TILES))
+        load_values(0)
+        load_tokens(q_raw, qw, 0, range(1, Q_TILES))
+        wo_view = Wo_vid.rearrange("(c u p e) n -> p (c u) (e n)", c=F_PASSES, u=2, e=2)
+        for c in range(F_PASSES):
+            nc.sync.dma_start(out=wo_raw[:, 2 * c : 2 * c + 2, :], in_=wo_view[:, 2 * c : 2 * c + 2, :])
+        nc.sync.dma_start(out=bias_bc[:], in_=bo_vid.partition_broadcast(P))
+        load_tokens(k_raw, kw, 1, range(Q_TILES))
+        load_tokens(q_raw, qw, 1, range(Q_TILES))
+        load_values(1)
+
+        kT = [keep.tile([P, NH, WIN_LEN], BF16, name="kT%d" % n) for n in range(N_WIN)]
+        v_codes = [keep.tile([P, INNER], U32, name="v_codes%d" % n, align_bytes=64) for n in range(N_WIN)]
+        v_scales = [keep.tile([P, INNER], U8, name="v_scales%d" % n, align_bytes=64) for n in range(N_WIN)]
+        wo_codes = keep.tile([P, F_PASSES, VID_DIM], U32, name="wo_codes", align_bytes=64)
+        wo_scales = keep.tile([P, F_PASSES, VID_DIM], U8, name="wo_scales", align_bytes=64)
+
+        out_rows = out.rearrange("(th n w) c -> n th w c", n=N_WIN, w=8)
+
+        qT = {}
+        e_sb = {}
+        stats = {}
+        e_grouped = {}
+        e_mx = {}
+        x_sb = {}
+        x_grouped = {}
+        x_mx = {}
+        grouped = {}
+
+        def transpose_q(t):
+            n, qt = divmod(t, Q_TILES)
+            qT_ps = aux_banks.tile([P, NH, P], BF16, name="qT_ps", tag="aux")
+            for g in range(NH):
+                nc.tensor.transpose(qT_ps[:, g, :], q_raw[n][:, qt, g * HD : (g + 1) * HD], ident_bf[:])
+            qT[t] = work.tile([P, NH, P], BF16, name="qT", tag="qT")
+            nc.scalar.copy(out=qT[t][:], in_=qT_ps[:])
+
+        def transpose_k(n, pair):
+            kT_ps = aux_banks.tile([P, 2, Q_TILES, P], BF16, name="kT_ps", tag="aux")
+            for h in range(2):
+                g = 2 * pair + h
+                for kt in range(Q_TILES):
+                    nc.tensor.transpose(kT_ps[:, h, kt, :], k_raw[n][:, kt, g * HD : (g + 1) * HD], ident_bf[:])
+            nc.scalar.copy(
+                out=kT[n][:, 2 * pair : 2 * pair + 2, :], in_=kT_ps[:].rearrange("p h t k -> p h (t k)")
+            )
+
+        def regroup(key, rows):
+            grouped[key] = work.tile([P, BANK, 4], BF16, name="grouped", tag="grouped", align_bytes=64)
+            nc.vector.tensor_copy(out=grouped[key][:], in_=rows.rearrange("p t f -> p f t"))
+
+        def quantise_grouped(key, codes, scales):
+            nc.vector.quantize_mx(
+                out=codes.bitcast(FP8X4), scales=scales, in_=grouped[key][:].rearrange("p f t -> p (f t)")
+            )
+
+        def scores(i):
+            t, g = divmod(i, NH)
+            n = t // Q_TILES
+            k, col = divmod(i, 4)
+            if col == 0:
+                stats[k] = {
+                    "max": work.tile([P, 4], F32, name="row_max", tag="row_max", bufs=4),
+                    "bias": work.tile([P, 4], F32, name="exp_bias", tag="exp_bias", bufs=4),
+                    "sum": work.tile([P, 4], F32, name="row_sum", tag="row_sum", bufs=4),
+                }
+            st = stats[k]
+            s_ps = s_banks.tile([P, WIN_LEN], F32, name="s_ps", tag="s")
+            nc.tensor.matmul(s_ps[:], lhsT=qT[t][:, g, :], rhs=kT[n][:, g, :], start=True, stop=True)
+            nc.vector.tensor_reduce(
+                out=st["max"][:, col : col + 1], in_=s_ps[:], axis=mybir.AxisListType.X, op=ALU.max
+            )
+            nc.gpsimd.tensor_scalar(
+                out=st["bias"][:, col : col + 1],
+                in0=st["max"][:, col : col + 1],
+                scalar1=-SCALE,
+                scalar2=0.0,
+                op0=ALU.mult,
+                op1=ALU.add,
+            )
+            e_sb[i] = work.tile([P, WIN_LEN], BF16, name="e_sb", tag="e_sb", bufs=8)
+            nc.scalar.activation(
+                out=e_sb[i][:],
+                in_=s_ps[:],
+                func=ACT.Exp,
+                bias=st["bias"][:, col : col + 1],
+                scale=SCALE,
+                accum_out=st["sum"][:, col : col + 1],
+            )
+
+        def flip_e(j):
+            k, half = divmod(j, 2)
+            if half == 0:
+                e_grouped[k] = work.tile([P, 4 * WIN_LEN], BF16, name="e_grouped", tag="e_grouped", bufs=3, align_bytes=64)
+            eT_ps = aux_banks.tile([P, 2, 2, P], F32, name="eT_ps", tag="aux")
+            for h in range(2):
+                words = e_sb[2 * j + h][:].bitcast(F32)
+                for u in range(2):
+                    nc.tensor.transpose(eT_ps[:, h, u, :], words[:, u * P : (u + 1) * P], ident_f32[:])
+            dst = e_grouped[k][:].bitcast(F32).rearrange("p (h q u) -> p h q u", h=4, u=2)
+            nc.scalar.copy(out=dst[:, 2 * half : 2 * half + 2, :, :], in_=eT_ps[:].rearrange("p h u q -> p h q u"))
+
+        def invert_sums(k):
+            stats[k]["inv"] = work.tile([P, 4], F32, name="inv_sum", tag="inv_sum", bufs=3)
+            nc.vector.reciprocal(out=stats[k]["inv"][:], in_=stats[k]["sum"][:])
+
+        def quantise_e(k):
+            codes = work.tile([P, WIN_LEN], U32, name="e_codes", tag="e_codes", align_bytes=64)
+            scales = work.tile([P, WIN_LEN], U8, name="e_scales", tag="e_scales", align_bytes=64)
+            nc.vector.quantize_mx(out=codes[:].bitcast(FP8X4), scales=scales[:], in_=e_grouped[k][:])
+            e_mx[k] = (codes, scales)
+
+        def attend(k):
+            t, half = divmod(k, 2)
+            n = t // Q_TILES
+            codes, scales = e_mx[k]
+            o_ps = aux_banks.tile([P, 4, HD], F32, name="o_ps", tag="aux")
+            for h in range(4):
+                q_cols = slice(h * P, (h + 1) * P)
+                d_cols = slice((4 * half + h) * HD, (4 * half + h + 1) * HD)
+                nc.tensor.matmul_mx(
+                    out=o_ps[:, h, :],
+                    lhsT=codes[:, q_cols].bitcast(FP8X4),
+                    lhsT_scale=scales[:, q_cols],
+                    rhs=v_codes[n][:, d_cols].bitcast(FP8X4),
+                    rhs_scale=v_scales[n][:, d_cols],
+                    start=True,
+                    stop=True,
+                )
+            if half == 0:
+                x_sb[t] = work.tile([P, INNER], BF16, name="x_sb", tag="x_sb")
+            nc.vector.tensor_tensor(
+                out=x_sb[t][:, half * 4 * HD : (half + 1) * 4 * HD].rearrange("p (h d) -> p h d", h=4),
+                in0=o_ps[:],
+                in1=stats[k]["inv"][:].unsqueeze(2).to_broadcast([P, 4, HD]),
+                op=ALU.mult,
+            )
+
+        def flip_x(t):
+            xT_ps = aux_banks.tile([P, 2 * F_PASSES, P], F32, name="xT_ps", tag="aux")
+            words = x_sb[t][:].bitcast(F32)
+            for cu in range(2 * F_PASSES):
+                nc.tensor.transpose(xT_ps[:, cu, :], words[:, cu * P : (cu + 1) * P], ident_f32[:])
+            x_grouped[t] = work.tile([P, F_PASSES * P * 4], BF16, name="x_grouped", tag="x_grouped", align_bytes=64)
+            nc.scalar.copy(
+                out=x_grouped[t][:].bitcast(F32).rearrange("p (c q u) -> p c q u", c=F_PASSES, u=2),
+                in_=xT_ps[:].rearrange("p (c u) q -> p c q u", u=2),
+            )
+
+        def quantise_x(t):
+            codes = work.tile([P, F_PASSES * P], U32, name="x_codes", tag="x_codes", align_bytes=64)
+            scales = work.tile([P, F_PASSES * P], U8, name="x_scales", tag="x_scales", align_bytes=64)
+            nc.vector.quantize_mx(out=codes[:].bitcast(FP8X4), scales=scales[:], in_=x_grouped[t][:])
+            x_mx[t] = (codes, scales)
+
+        def project(t, b):
+            n, qt = divmod(t, Q_TILES)
+            codes, scales = x_mx[t]
+            cols = slice(b * BANK, (b + 1) * BANK)
+            y_ps = aux_banks.tile([P, BANK], F32, name="y_ps", tag="aux")
+            for c in range(F_PASSES):
+                toks = slice(c * P, (c + 1) * P)
+                nc.tensor.matmul_mx(
+                    out=y_ps[:],
+                    lhsT=codes[:, toks].bitcast(FP8X4),
+                    lhsT_scale=scales[:, toks],
+                    rhs=wo_codes[:, c, cols].bitcast(FP8X4),
+                    rhs_scale=wo_scales[:, c, cols],
+                    start=(c == 0),
+                    stop=(c == F_PASSES - 1),
+                )
+            y_sb = work.tile([P, BANK], F32, name="y_sb", tag="y_sb", bufs=4)
+            nc.vector.tensor_tensor(out=y_sb[:], in0=y_ps[:], in1=bias_bc[:, cols], op=ALU.add)
+            nc.sync.dma_start(out=out_rows[n, qt * 16 : (qt + 1) * 16, :, cols], in_=y_sb[:])
+
+        v_rows = [v_raw[n][:].rearrange("p u (e f) -> p (u e) f", e=2) for n in range(N_WIN)]
+        wo_rows = wo_raw[:].rearrange("p (c u) (e n) -> p c (u e) n", u=2, e=2)
+
+        for step in range(-PREP_LEAD, N_STEPS + PROJECT_LAG + OUT_BANKS):
+            if 0 <= step < N_STEPS:
+                scores(step)
+
+            ahead = step + PREP_LEAD
+            if ahead < N_STEPS and ahead % NH == 0:
+                transpose_q(ahead // NH)
+            if ahead < N_STEPS and ahead % (NH * Q_TILES) < NH and ahead % 2 == 0:
+                transpose_k(ahead // (NH * Q_TILES), (ahead % NH) // 2)
+
+            n, in_window = divmod(step, NH * Q_TILES)
+            if 0 <= step < N_STEPS and 2 <= in_window < 6:
+                half, turn = divmod(in_window - 2, 2)
+                cols = slice(half * BANK, (half + 1) * BANK)
+                if turn == 0:
+                    regroup(("v", n, half), v_rows[n][:, :, cols])
+                else:
+                    quantise_grouped(("v", n, half), v_codes[n][:, cols], v_scales[n][:, cols])
+            if 6 <= step < 6 + 2 * F_PASSES * OUT_BANKS:
+                chunk, turn = divmod(step - 6, 2)
+                c, b = divmod(chunk, OUT_BANKS)
+                cols = slice(b * BANK, (b + 1) * BANK)
+                if turn == 0:
+                    regroup(("wo", c, b), wo_rows[:, c, :, cols])
+                else:
+                    quantise_grouped(("wo", c, b), wo_codes[:, c, cols], wo_scales[:, c, cols])
+
+            i = step - FLIP_LAG
+            if 0 <= i < N_STEPS and i % 2 == 1:
+                flip_e(i // 2)
+            i = step - RECIP_LAG
+            if 0 <= i < N_STEPS and i % 4 == 3:
+                invert_sums(i // 4)
+            i = step - QUANT_LAG
+            if 0 <= i < N_STEPS and i % 4 == 3:
+                quantise_e(i // 4)
+            i = step - ATTEND_LAG
+            if 0 <= i < N_STEPS and i % 4 == 3:
+                attend(i // 4)
+            i = step - XFLIP_LAG
+            if 0 <= i < N_STEPS and i % NH == NH - 1:
+                flip_x(i // NH)
+            i = step - XQUANT_LAG
+            if 0 <= i < N_STEPS and i % NH == NH - 1:
+                quantise_x(i // NH)
+            for b in range(OUT_BANKS):
+                i = step - PROJECT_LAG - b
+                if 0 <= i < N_STEPS and i % NH == NH - 1:
+                    project(i // NH, b)

@@ -46,7 +46,6 @@ def tile_naswinattention_pb_kernel(tc, qw, kw, vw, Wo_vid, bo_vid, out):
         work = ctx.enter_context(tc.tile_pool(name="work", bufs=2))
         s_banks = ctx.enter_context(tc.psum_pool(name="s_banks", bufs=4))
         aux_banks = ctx.enter_context(tc.psum_pool(name="aux_banks", bufs=4))
-        ctx.enter_context(tc.manual_schedule())
 
         ident_bf = keep.tile([P, P], BF16, name="ident_bf")
         make_identity(nc, ident_bf[:])

@@ -20,7 +20,8 @@ INNER = NH * HD
 VID_DIM = 1536
 Q_TILES = WIN_LEN // P
 N_TILES = N_WIN * Q_TILES
-N_STEPS = N_TILES * NH
+N_UNITS = N_TILES * NH
+WIN_UNITS = Q_TILES * NH
 K_PASS = 512
 F_PASSES = INNER // K_PASS
 BANK = 512
@@ -29,14 +30,37 @@ SCALE = 1.0 / (HD ** 0.5)
 
 FLOPS = 2 * 2 * N_WIN * NH * WIN_LEN * WIN_LEN * HD + 2 * N_WIN * WIN_LEN * INNER * VID_DIM
 
-PREP_LEAD = 2
-FLIP_LAG = 4
-RECIP_LAG = 5
-QUANT_LAG = 8
-ATTEND_LAG = 9
-XFLIP_LAG = 10
-XQUANT_LAG = 14
-PROJECT_LAG = 15
+AT_TRANSPOSE_QK = -4
+AT_COPY_QK = -3
+AT_SCORES = -1
+AT_MAX = 0
+AT_EXP = 1
+AT_FLIP_E = 3
+AT_COPY_E = 4
+AT_QUANT_E = 5
+AT_ATTEND = 6
+AT_SCALE_O = 7
+AT_FLIP_X = 8
+AT_COPY_X = 9
+AT_QUANT_X = 10
+AT_PROJECT = 11
+AT_BIAS = 12
+FIRST_STEP = AT_TRANSPOSE_QK
+LAST_STEP = N_UNITS - 1 + AT_BIAS + OUT_BANKS - 1
+V_STEP = 1
+WO_STEP = 5
+
+
+def starts(i, size):
+    if 0 <= i < N_UNITS and i % size == 0:
+        return i // size
+    return None
+
+
+def ends(i, size):
+    if 0 <= i < N_UNITS and i % size == size - 1:
+        return i // size
+    return None
 
 
 def tile_naswinattention_pb_kernel(tc, qw, kw, vw, Wo_vid, bo_vid, out):
@@ -44,8 +68,8 @@ def tile_naswinattention_pb_kernel(tc, qw, kw, vw, Wo_vid, bo_vid, out):
     with ExitStack() as ctx:
         keep = ctx.enter_context(tc.tile_pool(name="keep", bufs=1))
         work = ctx.enter_context(tc.tile_pool(name="work", bufs=2))
-        s_banks = ctx.enter_context(tc.psum_pool(name="s_banks", bufs=4))
-        aux_banks = ctx.enter_context(tc.psum_pool(name="aux_banks", bufs=4))
+        s_banks = ctx.enter_context(tc.psum_pool(name="s_banks", bufs=3))
+        aux_banks = ctx.enter_context(tc.psum_pool(name="aux_banks", bufs=5))
 
         ident_bf = keep.tile([P, P], BF16, name="ident_bf")
         make_identity(nc, ident_bf[:])
@@ -58,26 +82,32 @@ def tile_naswinattention_pb_kernel(tc, qw, kw, vw, Wo_vid, bo_vid, out):
         wo_raw = keep.tile([P, 2 * F_PASSES, 2 * VID_DIM], BF16, name="wo_raw")
         bias_bc = keep.tile([P, VID_DIM], BF16, name="bias_bc")
 
-        def load_tokens(dst, src, n, tiles):
-            view = src[n].rearrange("(t p) g d -> p t (g d)", p=P)
+        def load_queries(n, tiles):
+            view = qw[n].rearrange("(t p) g d -> p t (g d)", p=P)
             for t in tiles:
-                nc.sync.dma_start(out=dst[n][:, t, :], in_=view[:, t, :])
+                nc.sync.dma_start(out=q_raw[n][:, t, :], in_=view[:, t, :])
+
+        def load_keys(n):
+            view = kw[n].rearrange("(t p) g d -> p t (g d)", p=P)
+            for pair in range(NH // 2):
+                cols = slice(2 * pair * HD, (2 * pair + 2) * HD)
+                nc.sync.dma_start(out=k_raw[n][:, :, cols], in_=view[:, :, cols])
 
         def load_values(n):
             nc.sync.dma_start(
                 out=v_raw[n][:], in_=vw[n].rearrange("(u p e) g d -> p u (e g d)", u=2, e=2)
             )
 
-        load_tokens(q_raw, qw, 0, [0])
-        load_tokens(k_raw, kw, 0, range(Q_TILES))
+        load_queries(0, [0])
+        load_keys(0)
         load_values(0)
-        load_tokens(q_raw, qw, 0, range(1, Q_TILES))
+        load_queries(0, range(1, Q_TILES))
         wo_view = Wo_vid.rearrange("(c u p e) n -> p (c u) (e n)", c=F_PASSES, u=2, e=2)
         for c in range(F_PASSES):
             nc.sync.dma_start(out=wo_raw[:, 2 * c : 2 * c + 2, :], in_=wo_view[:, 2 * c : 2 * c + 2, :])
         nc.sync.dma_start(out=bias_bc[:], in_=bo_vid.partition_broadcast(P))
-        load_tokens(k_raw, kw, 1, range(Q_TILES))
-        load_tokens(q_raw, qw, 1, range(Q_TILES))
+        load_keys(1)
+        load_queries(1, range(Q_TILES))
         load_values(1)
 
         kT = [keep.tile([P, NH, WIN_LEN], BF16, name="kT%d" % n) for n in range(N_WIN)]
@@ -86,39 +116,44 @@ def tile_naswinattention_pb_kernel(tc, qw, kw, vw, Wo_vid, bo_vid, out):
         wo_codes = keep.tile([P, F_PASSES, VID_DIM], U32, name="wo_codes", align_bytes=64)
         wo_scales = keep.tile([P, F_PASSES, VID_DIM], U8, name="wo_scales", align_bytes=64)
 
+        v_rows = [v_raw[n][:].rearrange("p u (e f) -> p (u e) f", e=2) for n in range(N_WIN)]
+        wo_rows = wo_raw[:].rearrange("p (c u) (e n) -> p c (u e) n", u=2, e=2)
         out_rows = out.rearrange("(th n w) c -> n th w c", n=N_WIN, w=8)
 
-        qT = {}
-        e_sb = {}
-        stats = {}
-        e_grouped = {}
-        e_mx = {}
-        x_sb = {}
-        x_grouped = {}
-        x_mx = {}
+        qT_ps, qT, kT_ps, s_ps, e_sb, eT_ps = {}, {}, {}, {}, {}, {}
+        row_max, exp_bias, row_sum, inv_sum = {}, {}, {}, {}
+        e_grouped, e_codes, e_scales, o_ps = {}, {}, {}, {}
+        x_sb, xT_ps, x_grouped, x_codes, x_scales, y_ps = {}, {}, {}, {}, {}, {}
         grouped = {}
 
         def transpose_q(t):
             n, qt = divmod(t, Q_TILES)
-            qT_ps = aux_banks.tile([P, NH, P], BF16, name="qT_ps", tag="aux")
+            qT_ps[t] = aux_banks.tile([P, NH, P], BF16, name="qT_ps", tag="aux")
             for g in range(NH):
-                nc.tensor.transpose(qT_ps[:, g, :], q_raw[n][:, qt, g * HD : (g + 1) * HD], ident_bf[:])
+                nc.tensor.transpose(qT_ps[t][:, g, :], q_raw[n][:, qt, g * HD : (g + 1) * HD], ident_bf[:])
+
+        def copy_qT(t):
             qT[t] = work.tile([P, NH, P], BF16, name="qT", tag="qT")
-            nc.scalar.copy(out=qT[t][:], in_=qT_ps[:])
+            nc.scalar.copy(out=qT[t][:], in_=qT_ps[t][:])
 
         def transpose_k(n, pair):
-            kT_ps = aux_banks.tile([P, 2, Q_TILES, P], BF16, name="kT_ps", tag="aux")
+            kT_ps[n, pair] = aux_banks.tile([P, 2, Q_TILES, P], BF16, name="kT_ps", tag="aux")
             for h in range(2):
                 g = 2 * pair + h
                 for kt in range(Q_TILES):
-                    nc.tensor.transpose(kT_ps[:, h, kt, :], k_raw[n][:, kt, g * HD : (g + 1) * HD], ident_bf[:])
+                    nc.tensor.transpose(kT_ps[n, pair][:, h, kt, :], k_raw[n][:, kt, g * HD : (g + 1) * HD], ident_bf[:])
+
+        def copy_kT(n, pair):
             nc.scalar.copy(
-                out=kT[n][:, 2 * pair : 2 * pair + 2, :], in_=kT_ps[:].rearrange("p h t k -> p h (t k)")
+                out=kT[n][:, 2 * pair : 2 * pair + 2, :], in_=kT_ps[n, pair][:].rearrange("p h t k -> p h (t k)")
             )
 
         def regroup(key, rows):
             grouped[key] = work.tile([P, BANK, 4], BF16, name="grouped", tag="grouped", align_bytes=64)
-            nc.vector.tensor_copy(out=grouped[key][:], in_=rows.rearrange("p t f -> p f t"))
+            nc.vector.tensor_copy(
+                out=grouped[key][:].rearrange("p (c i) t -> p c t i", i=4),
+                in_=rows.rearrange("p t (c i) -> p c t i", i=4),
+            )
 
         def quantise_grouped(key, codes, scales):
             nc.vector.quantize_mx(
@@ -127,146 +162,157 @@ def tile_naswinattention_pb_kernel(tc, qw, kw, vw, Wo_vid, bo_vid, out):
 
         def scores(i):
             t, g = divmod(i, NH)
-            n = t // Q_TILES
+            s_ps[i] = s_banks.tile([P, WIN_LEN], F32, name="s_ps", tag="s")
+            nc.tensor.matmul(s_ps[i][:], lhsT=qT[t][:, g, :], rhs=kT[t // Q_TILES][:, g, :], start=True, stop=True)
+
+        def maximum(i):
             k, col = divmod(i, 4)
             if col == 0:
-                stats[k] = {
-                    "max": work.tile([P, 4], F32, name="row_max", tag="row_max", bufs=4),
-                    "bias": work.tile([P, 4], F32, name="exp_bias", tag="exp_bias", bufs=4),
-                    "sum": work.tile([P, 4], F32, name="row_sum", tag="row_sum", bufs=4),
-                }
-            st = stats[k]
-            s_ps = s_banks.tile([P, WIN_LEN], F32, name="s_ps", tag="s")
-            nc.tensor.matmul(s_ps[:], lhsT=qT[t][:, g, :], rhs=kT[n][:, g, :], start=True, stop=True)
+                row_max[k] = work.tile([P, 4], F32, name="row_max", tag="row_max", bufs=4)
+                exp_bias[k] = work.tile([P, 4], F32, name="exp_bias", tag="exp_bias", bufs=4)
             nc.vector.tensor_reduce(
-                out=st["max"][:, col : col + 1], in_=s_ps[:], axis=mybir.AxisListType.X, op=ALU.max
+                out=row_max[k][:, col : col + 1], in_=s_ps[i][:], axis=mybir.AxisListType.X, op=ALU.max
             )
             nc.gpsimd.tensor_scalar(
-                out=st["bias"][:, col : col + 1],
-                in0=st["max"][:, col : col + 1],
+                out=exp_bias[k][:, col : col + 1],
+                in0=row_max[k][:, col : col + 1],
                 scalar1=-SCALE,
                 scalar2=0.0,
                 op0=ALU.mult,
                 op1=ALU.add,
             )
+
+        def exponential(i):
+            k, col = divmod(i, 4)
+            if col == 0:
+                row_sum[k] = work.tile([P, 4], F32, name="row_sum", tag="row_sum", bufs=4)
             e_sb[i] = work.tile([P, WIN_LEN], BF16, name="e_sb", tag="e_sb", bufs=8)
             nc.scalar.activation(
                 out=e_sb[i][:],
-                in_=s_ps[:],
+                in_=s_ps[i][:],
                 func=ACT.Exp,
-                bias=st["bias"][:, col : col + 1],
+                bias=exp_bias[k][:, col : col + 1],
                 scale=SCALE,
-                accum_out=st["sum"][:, col : col + 1],
+                accum_out=row_sum[k][:, col : col + 1],
             )
 
         def flip_e(j):
-            k, half = divmod(j, 2)
-            if half == 0:
-                e_grouped[k] = work.tile([P, 4 * WIN_LEN], BF16, name="e_grouped", tag="e_grouped", bufs=3, align_bytes=64)
-            eT_ps = aux_banks.tile([P, 2, 2, P], F32, name="eT_ps", tag="aux")
+            eT_ps[j] = aux_banks.tile([P, 2, 2, P], F32, name="eT_ps", tag="aux")
             for h in range(2):
                 words = e_sb[2 * j + h][:].bitcast(F32)
                 for u in range(2):
-                    nc.tensor.transpose(eT_ps[:, h, u, :], words[:, u * P : (u + 1) * P], ident_f32[:])
-            dst = e_grouped[k][:].bitcast(F32).rearrange("p (h q u) -> p h q u", h=4, u=2)
-            nc.scalar.copy(out=dst[:, 2 * half : 2 * half + 2, :, :], in_=eT_ps[:].rearrange("p h u q -> p h q u"))
+                    nc.tensor.transpose(eT_ps[j][:, h, u, :], words[:, u * P : (u + 1) * P], ident_f32[:])
 
-        def invert_sums(k):
-            stats[k]["inv"] = work.tile([P, 4], F32, name="inv_sum", tag="inv_sum", bufs=3)
-            nc.vector.reciprocal(out=stats[k]["inv"][:], in_=stats[k]["sum"][:])
+        def copy_eT(j):
+            k, half = divmod(j, 2)
+            if half == 0:
+                e_grouped[k] = work.tile([P, 4 * WIN_LEN], BF16, name="e_grouped", tag="e_grouped", bufs=3, align_bytes=64)
+            dst = e_grouped[k][:].bitcast(F32).rearrange("p (h q u) -> p h q u", h=4, u=2)
+            nc.scalar.copy(out=dst[:, 2 * half : 2 * half + 2, :, :], in_=eT_ps[j][:].rearrange("p h u q -> p h q u"))
 
         def quantise_e(k):
-            codes = work.tile([P, WIN_LEN], U32, name="e_codes", tag="e_codes", align_bytes=64)
-            scales = work.tile([P, WIN_LEN], U8, name="e_scales", tag="e_scales", align_bytes=64)
-            nc.vector.quantize_mx(out=codes[:].bitcast(FP8X4), scales=scales[:], in_=e_grouped[k][:])
-            e_mx[k] = (codes, scales)
+            inv_sum[k] = work.tile([P, 4], F32, name="inv_sum", tag="inv_sum", bufs=3)
+            nc.vector.reciprocal(out=inv_sum[k][:], in_=row_sum[k][:])
+            e_codes[k] = work.tile([P, WIN_LEN], U32, name="e_codes", tag="e_codes", align_bytes=64)
+            e_scales[k] = work.tile([P, WIN_LEN], U8, name="e_scales", tag="e_scales", align_bytes=64)
+            nc.vector.quantize_mx(out=e_codes[k][:].bitcast(FP8X4), scales=e_scales[k][:], in_=e_grouped[k][:])
 
         def attend(k):
             t, half = divmod(k, 2)
             n = t // Q_TILES
-            codes, scales = e_mx[k]
-            o_ps = aux_banks.tile([P, 4, HD], F32, name="o_ps", tag="aux")
+            o_ps[k] = aux_banks.tile([P, 4, HD], F32, name="o_ps", tag="aux")
             for h in range(4):
                 q_cols = slice(h * P, (h + 1) * P)
                 d_cols = slice((4 * half + h) * HD, (4 * half + h + 1) * HD)
                 nc.tensor.matmul_mx(
-                    out=o_ps[:, h, :],
-                    lhsT=codes[:, q_cols].bitcast(FP8X4),
-                    lhsT_scale=scales[:, q_cols],
+                    out=o_ps[k][:, h, :],
+                    lhsT=e_codes[k][:, q_cols].bitcast(FP8X4),
+                    lhsT_scale=e_scales[k][:, q_cols],
                     rhs=v_codes[n][:, d_cols].bitcast(FP8X4),
                     rhs_scale=v_scales[n][:, d_cols],
                     start=True,
                     stop=True,
                 )
+
+        def scale_o(k):
+            t, half = divmod(k, 2)
             if half == 0:
                 x_sb[t] = work.tile([P, INNER], BF16, name="x_sb", tag="x_sb")
-            nc.vector.tensor_tensor(
-                out=x_sb[t][:, half * 4 * HD : (half + 1) * 4 * HD].rearrange("p (h d) -> p h d", h=4),
-                in0=o_ps[:],
-                in1=stats[k]["inv"][:].unsqueeze(2).to_broadcast([P, 4, HD]),
-                op=ALU.mult,
-            )
+            for h in range(4):
+                d_cols = slice((4 * half + h) * HD, (4 * half + h + 1) * HD)
+                nc.scalar.activation(
+                    out=x_sb[t][:, d_cols], in_=o_ps[k][:, h, :], func=ACT.Copy, scale=inv_sum[k][:, h : h + 1]
+                )
 
         def flip_x(t):
-            xT_ps = aux_banks.tile([P, 2 * F_PASSES, P], F32, name="xT_ps", tag="aux")
+            xT_ps[t] = aux_banks.tile([P, 2 * F_PASSES, P], F32, name="xT_ps", tag="aux")
             words = x_sb[t][:].bitcast(F32)
             for cu in range(2 * F_PASSES):
-                nc.tensor.transpose(xT_ps[:, cu, :], words[:, cu * P : (cu + 1) * P], ident_f32[:])
+                nc.tensor.transpose(xT_ps[t][:, cu, :], words[:, cu * P : (cu + 1) * P], ident_f32[:])
+
+        def copy_xT(t):
             x_grouped[t] = work.tile([P, F_PASSES * P * 4], BF16, name="x_grouped", tag="x_grouped", align_bytes=64)
             nc.scalar.copy(
                 out=x_grouped[t][:].bitcast(F32).rearrange("p (c q u) -> p c q u", c=F_PASSES, u=2),
-                in_=xT_ps[:].rearrange("p (c u) q -> p c q u", u=2),
+                in_=xT_ps[t][:].rearrange("p (c u) q -> p c q u", u=2),
             )
 
         def quantise_x(t):
-            codes = work.tile([P, F_PASSES * P], U32, name="x_codes", tag="x_codes", align_bytes=64)
-            scales = work.tile([P, F_PASSES * P], U8, name="x_scales", tag="x_scales", align_bytes=64)
-            nc.vector.quantize_mx(out=codes[:].bitcast(FP8X4), scales=scales[:], in_=x_grouped[t][:])
-            x_mx[t] = (codes, scales)
+            x_codes[t] = work.tile([P, F_PASSES * P], U32, name="x_codes", tag="x_codes", align_bytes=64)
+            x_scales[t] = work.tile([P, F_PASSES * P], U8, name="x_scales", tag="x_scales", align_bytes=64)
+            nc.vector.quantize_mx(out=x_codes[t][:].bitcast(FP8X4), scales=x_scales[t][:], in_=x_grouped[t][:])
 
         def project(t, b):
-            n, qt = divmod(t, Q_TILES)
-            codes, scales = x_mx[t]
             cols = slice(b * BANK, (b + 1) * BANK)
-            y_ps = aux_banks.tile([P, BANK], F32, name="y_ps", tag="aux")
+            y_ps[t, b] = aux_banks.tile([P, BANK], F32, name="y_ps", tag="aux")
             for c in range(F_PASSES):
                 toks = slice(c * P, (c + 1) * P)
                 nc.tensor.matmul_mx(
-                    out=y_ps[:],
-                    lhsT=codes[:, toks].bitcast(FP8X4),
-                    lhsT_scale=scales[:, toks],
+                    out=y_ps[t, b][:],
+                    lhsT=x_codes[t][:, toks].bitcast(FP8X4),
+                    lhsT_scale=x_scales[t][:, toks],
                     rhs=wo_codes[:, c, cols].bitcast(FP8X4),
                     rhs_scale=wo_scales[:, c, cols],
                     start=(c == 0),
                     stop=(c == F_PASSES - 1),
                 )
+
+        def add_bias_and_store(t, b):
+            n, qt = divmod(t, Q_TILES)
+            cols = slice(b * BANK, (b + 1) * BANK)
             y_sb = work.tile([P, BANK], F32, name="y_sb", tag="y_sb", bufs=4)
-            nc.vector.tensor_tensor(out=y_sb[:], in0=y_ps[:], in1=bias_bc[:, cols], op=ALU.add)
+            nc.vector.tensor_tensor(out=y_sb[:], in0=y_ps[t, b][:], in1=bias_bc[:, cols], op=ALU.add)
             nc.sync.dma_start(out=out_rows[n, qt * 16 : (qt + 1) * 16, :, cols], in_=y_sb[:])
 
-        v_rows = [v_raw[n][:].rearrange("p u (e f) -> p (u e) f", e=2) for n in range(N_WIN)]
-        wo_rows = wo_raw[:].rearrange("p (c u) (e n) -> p c (u e) n", u=2, e=2)
+        for step in range(FIRST_STEP, LAST_STEP + 1):
+            i = step - AT_TRANSPOSE_QK
+            if starts(i, NH) is not None:
+                transpose_q(i // NH)
+            if starts(i, 2) is not None and i % WIN_UNITS < NH:
+                transpose_k(i // WIN_UNITS, (i % NH) // 2)
+            i = step - AT_COPY_QK
+            if starts(i, NH) is not None:
+                copy_qT(i // NH)
+            if starts(i, 2) is not None and i % WIN_UNITS < NH:
+                copy_kT(i // WIN_UNITS, (i % NH) // 2)
 
-        for step in range(-PREP_LEAD, N_STEPS + PROJECT_LAG + OUT_BANKS):
-            if 0 <= step < N_STEPS:
-                scores(step)
+            if 0 <= step - AT_SCORES < N_UNITS:
+                scores(step - AT_SCORES)
+            if 0 <= step - AT_MAX < N_UNITS:
+                maximum(step - AT_MAX)
+            if 0 <= step - AT_EXP < N_UNITS:
+                exponential(step - AT_EXP)
 
-            ahead = step + PREP_LEAD
-            if ahead < N_STEPS and ahead % NH == 0:
-                transpose_q(ahead // NH)
-            if ahead < N_STEPS and ahead % (NH * Q_TILES) < NH and ahead % 2 == 0:
-                transpose_k(ahead // (NH * Q_TILES), (ahead % NH) // 2)
-
-            n, in_window = divmod(step, NH * Q_TILES)
-            if 0 <= step < N_STEPS and 2 <= in_window < 6:
-                half, turn = divmod(in_window - 2, 2)
+            n, in_window = divmod(step, WIN_UNITS)
+            if 0 <= step < N_UNITS and V_STEP <= in_window < V_STEP + 4:
+                half, turn = divmod(in_window - V_STEP, 2)
                 cols = slice(half * BANK, (half + 1) * BANK)
                 if turn == 0:
                     regroup(("v", n, half), v_rows[n][:, :, cols])
                 else:
                     quantise_grouped(("v", n, half), v_codes[n][:, cols], v_scales[n][:, cols])
-            if 6 <= step < 6 + 2 * F_PASSES * OUT_BANKS:
-                chunk, turn = divmod(step - 6, 2)
+            if WO_STEP <= step < WO_STEP + 2 * F_PASSES * OUT_BANKS:
+                chunk, turn = divmod(step - WO_STEP, 2)
                 c, b = divmod(chunk, OUT_BANKS)
                 cols = slice(b * BANK, (b + 1) * BANK)
                 if turn == 0:
@@ -274,25 +320,34 @@ def tile_naswinattention_pb_kernel(tc, qw, kw, vw, Wo_vid, bo_vid, out):
                 else:
                     quantise_grouped(("wo", c, b), wo_codes[:, c, cols], wo_scales[:, c, cols])
 
-            i = step - FLIP_LAG
-            if 0 <= i < N_STEPS and i % 2 == 1:
-                flip_e(i // 2)
-            i = step - RECIP_LAG
-            if 0 <= i < N_STEPS and i % 4 == 3:
-                invert_sums(i // 4)
-            i = step - QUANT_LAG
-            if 0 <= i < N_STEPS and i % 4 == 3:
-                quantise_e(i // 4)
-            i = step - ATTEND_LAG
-            if 0 <= i < N_STEPS and i % 4 == 3:
-                attend(i // 4)
-            i = step - XFLIP_LAG
-            if 0 <= i < N_STEPS and i % NH == NH - 1:
-                flip_x(i // NH)
-            i = step - XQUANT_LAG
-            if 0 <= i < N_STEPS and i % NH == NH - 1:
-                quantise_x(i // NH)
+            j = ends(step - AT_FLIP_E, 2)
+            if j is not None:
+                flip_e(j)
+            j = ends(step - AT_COPY_E, 2)
+            if j is not None:
+                copy_eT(j)
+            k = ends(step - AT_QUANT_E, 4)
+            if k is not None:
+                quantise_e(k)
+            k = ends(step - AT_ATTEND, 4)
+            if k is not None:
+                attend(k)
+            k = ends(step - AT_SCALE_O, 4)
+            if k is not None:
+                scale_o(k)
+            t = ends(step - AT_FLIP_X, NH)
+            if t is not None:
+                flip_x(t)
+            t = ends(step - AT_COPY_X, NH)
+            if t is not None:
+                copy_xT(t)
+            t = ends(step - AT_QUANT_X, NH)
+            if t is not None:
+                quantise_x(t)
             for b in range(OUT_BANKS):
-                i = step - PROJECT_LAG - b
-                if 0 <= i < N_STEPS and i % NH == NH - 1:
-                    project(i // NH, b)
+                t = ends(step - AT_PROJECT - b, NH)
+                if t is not None:
+                    project(t, b)
+                t = ends(step - AT_BIAS - b, NH)
+                if t is not None:
+                    add_bias_and_store(t, b)

@@ -30,8 +30,8 @@ SCALE = 1.0 / (HD ** 0.5)
 
 FLOPS = 2 * 2 * N_WIN * NH * WIN_LEN * WIN_LEN * HD + 2 * N_WIN * WIN_LEN * INNER * VID_DIM
 
-AT_TRANSPOSE_QK = -4
-AT_COPY_QK = -3
+AT_TRANSPOSE_QK = -5
+AT_COPY_QK = -4
 AT_SCORES = -1
 AT_MAX = 0
 AT_EXP = 1
@@ -43,11 +43,12 @@ AT_SCALE_O = 7
 AT_FLIP_X = 8
 AT_COPY_X = 9
 AT_QUANT_X = 10
-AT_PROJECT = 11
-AT_BIAS = 12
+AT_PROJECT = 13
+AT_BIAS = 14
 FIRST_STEP = AT_TRANSPOSE_QK
 LAST_STEP = N_UNITS - 1 + AT_BIAS + OUT_BANKS - 1
-V_STEP = 1
+NEXT_K_STEP = 1
+V_STEPS = ((1, 2, 3, 4), (19, 27, 35, 43))
 WO_STEP = 5
 
 
@@ -70,6 +71,7 @@ def tile_naswinattention_pb_kernel(tc, qw, kw, vw, Wo_vid, bo_vid, out):
         work = ctx.enter_context(tc.tile_pool(name="work", bufs=2))
         s_banks = ctx.enter_context(tc.psum_pool(name="s_banks", bufs=3))
         aux_banks = ctx.enter_context(tc.psum_pool(name="aux_banks", bufs=5))
+        ctx.enter_context(tc.manual_schedule())
 
         ident_bf = keep.tile([P, P], BF16, name="ident_bf")
         make_identity(nc, ident_bf[:])
@@ -87,9 +89,9 @@ def tile_naswinattention_pb_kernel(tc, qw, kw, vw, Wo_vid, bo_vid, out):
             for t in tiles:
                 nc.sync.dma_start(out=q_raw[n][:, t, :], in_=view[:, t, :])
 
-        def load_keys(n):
+        def load_keys(n, pairs):
             view = kw[n].rearrange("(t p) g d -> p t (g d)", p=P)
-            for pair in range(NH // 2):
+            for pair in pairs:
                 cols = slice(2 * pair * HD, (2 * pair + 2) * HD)
                 nc.sync.dma_start(out=k_raw[n][:, :, cols], in_=view[:, :, cols])
 
@@ -98,17 +100,25 @@ def tile_naswinattention_pb_kernel(tc, qw, kw, vw, Wo_vid, bo_vid, out):
                 out=v_raw[n][:], in_=vw[n].rearrange("(u p e) g d -> p u (e g d)", u=2, e=2)
             )
 
+        def load_weights(c):
+            view = Wo_vid.rearrange("(c u p e) n -> p (c u) (e n)", c=F_PASSES, u=2, e=2)
+            nc.sync.dma_start(out=wo_raw[:, 2 * c : 2 * c + 2, :], in_=view[:, 2 * c : 2 * c + 2, :])
+
         load_queries(0, [0])
-        load_keys(0)
+        load_keys(0, range(NH // 2))
         load_values(0)
-        load_queries(0, range(1, Q_TILES))
-        wo_view = Wo_vid.rearrange("(c u p e) n -> p (c u) (e n)", c=F_PASSES, u=2, e=2)
-        for c in range(F_PASSES):
-            nc.sync.dma_start(out=wo_raw[:, 2 * c : 2 * c + 2, :], in_=wo_view[:, 2 * c : 2 * c + 2, :])
+        load_keys(1, [0])
+        load_queries(0, [1])
+        load_weights(0)
+        load_keys(1, [1])
+        load_weights(1)
+        load_queries(0, [2])
         nc.sync.dma_start(out=bias_bc[:], in_=bo_vid.partition_broadcast(P))
-        load_keys(1)
-        load_queries(1, range(Q_TILES))
+        load_keys(1, [2])
+        load_queries(0, [3])
+        load_keys(1, [3])
         load_values(1)
+        load_queries(1, range(Q_TILES))
 
         kT = [keep.tile([P, NH, WIN_LEN], BF16, name="kT%d" % n) for n in range(N_WIN)]
         v_codes = [keep.tile([P, INNER], U32, name="v_codes%d" % n, align_bytes=64) for n in range(N_WIN)]
@@ -149,7 +159,7 @@ def tile_naswinattention_pb_kernel(tc, qw, kw, vw, Wo_vid, bo_vid, out):
             )
 
         def regroup(key, rows):
-            grouped[key] = work.tile([P, BANK, 4], BF16, name="grouped", tag="grouped", align_bytes=64)
+            grouped[key] = work.tile([P, BANK, 4], BF16, name="grouped", tag="grouped_" + key[0], align_bytes=64)
             nc.vector.tensor_copy(
                 out=grouped[key][:].rearrange("p (c i) t -> p c t i", i=4),
                 in_=rows.rearrange("p t (c i) -> p c t i", i=4),
@@ -238,11 +248,18 @@ def tile_naswinattention_pb_kernel(tc, qw, kw, vw, Wo_vid, bo_vid, out):
             t, half = divmod(k, 2)
             if half == 0:
                 x_sb[t] = work.tile([P, INNER], BF16, name="x_sb", tag="x_sb")
-            for h in range(4):
-                d_cols = slice((4 * half + h) * HD, (4 * half + h + 1) * HD)
-                nc.scalar.activation(
-                    out=x_sb[t][:, d_cols], in_=o_ps[k][:, h, :], func=ACT.Copy, scale=inv_sum[k][:, h : h + 1]
+                nc.vector.tensor_tensor(
+                    out=x_sb[t][:, : 4 * HD].rearrange("p (h d) -> p h d", h=4),
+                    in0=o_ps[k][:],
+                    in1=inv_sum[k][:].unsqueeze(2).to_broadcast([P, 4, HD]),
+                    op=ALU.mult,
                 )
+            else:
+                for h in range(4):
+                    d_cols = slice((4 + h) * HD, (4 + h + 1) * HD)
+                    nc.scalar.activation(
+                        out=x_sb[t][:, d_cols], in_=o_ps[k][:, h, :], func=ACT.Copy, scale=inv_sum[k][:, h : h + 1]
+                    )
 
         def flip_x(t):
             xT_ps[t] = aux_banks.tile([P, 2 * F_PASSES, P], F32, name="xT_ps", tag="aux")
@@ -288,13 +305,18 @@ def tile_naswinattention_pb_kernel(tc, qw, kw, vw, Wo_vid, bo_vid, out):
             i = step - AT_TRANSPOSE_QK
             if starts(i, NH) is not None:
                 transpose_q(i // NH)
-            if starts(i, 2) is not None and i % WIN_UNITS < NH:
-                transpose_k(i // WIN_UNITS, (i % NH) // 2)
+            if starts(i, 2) is not None and i < NH:
+                transpose_k(0, i // 2)
             i = step - AT_COPY_QK
             if starts(i, NH) is not None:
                 copy_qT(i // NH)
-            if starts(i, 2) is not None and i % WIN_UNITS < NH:
-                copy_kT(i // WIN_UNITS, (i % NH) // 2)
+            if starts(i, 2) is not None and i < NH:
+                copy_kT(0, i // 2)
+            tile_no, tile_step = divmod(step, NH)
+            if 0 <= tile_no < Q_TILES and tile_step == NEXT_K_STEP:
+                transpose_k(1, tile_no)
+            if 0 <= tile_no < Q_TILES and tile_step == NEXT_K_STEP + 1:
+                copy_kT(1, tile_no)
 
             if 0 <= step - AT_SCORES < N_UNITS:
                 scores(step - AT_SCORES)
@@ -303,14 +325,14 @@ def tile_naswinattention_pb_kernel(tc, qw, kw, vw, Wo_vid, bo_vid, out):
             if 0 <= step - AT_EXP < N_UNITS:
                 exponential(step - AT_EXP)
 
-            n, in_window = divmod(step, WIN_UNITS)
-            if 0 <= step < N_UNITS and V_STEP <= in_window < V_STEP + 4:
-                half, turn = divmod(in_window - V_STEP, 2)
-                cols = slice(half * BANK, (half + 1) * BANK)
-                if turn == 0:
-                    regroup(("v", n, half), v_rows[n][:, :, cols])
-                else:
-                    quantise_grouped(("v", n, half), v_codes[n][:, cols], v_scales[n][:, cols])
+            for n in range(N_WIN):
+                if step in V_STEPS[n]:
+                    half, turn = divmod(V_STEPS[n].index(step), 2)
+                    cols = slice(half * BANK, (half + 1) * BANK)
+                    if turn == 0:
+                        regroup(("v", n, half), v_rows[n][:, :, cols])
+                    else:
+                        quantise_grouped(("v", n, half), v_codes[n][:, cols], v_scales[n][:, cols])
             if WO_STEP <= step < WO_STEP + 2 * F_PASSES * OUT_BANKS:
                 chunk, turn = divmod(step - WO_STEP, 2)
                 c, b = divmod(chunk, OUT_BANKS)

@@ -32,6 +32,8 @@ FLOPS = 2 * 2 * N_WIN * NH * WIN_LEN * WIN_LEN * HD + 2 * N_WIN * WIN_LEN * INNE
 
 AT_TRANSPOSE_QK = -5
 AT_COPY_QK = -4
+AT_TRANSPOSE_K = -3
+AT_COPY_K = -2
 AT_SCORES = -1
 AT_MAX = 0
 AT_EXP = 1
@@ -43,13 +45,12 @@ AT_SCALE_O = 7
 AT_FLIP_X = 8
 AT_COPY_X = 9
 AT_QUANT_X = 10
-AT_PROJECT = 13
-AT_BIAS = 14
 FIRST_STEP = AT_TRANSPOSE_QK
-LAST_STEP = N_UNITS - 1 + AT_BIAS + OUT_BANKS - 1
-NEXT_K_STEP = 1
-V_STEPS = ((1, 2, 3, 4), (19, 27, 35, 43))
-WO_STEP = 5
+NEXT_K_STEPS = (12, 18, 24, 30)
+V_SCALES = ()
+V1_FIRST = False
+V0_FIRST = 3
+PIECES = 2
 
 
 def starts(i, size):
@@ -96,28 +97,33 @@ def tile_naswinattention_pb_kernel(tc, qw, kw, vw, Wo_vid, bo_vid, out):
                 nc.sync.dma_start(out=k_raw[n][:, :, cols], in_=view[:, :, cols])
 
         def load_values(n):
-            nc.sync.dma_start(
-                out=v_raw[n][:], in_=vw[n].rearrange("(u p e) g d -> p u (e g d)", u=2, e=2)
-            )
+            view = vw[n].rearrange("(u p e) g d -> p u e (g d)", u=2, e=2)
+            tile_view = v_raw[n][:].rearrange("p u (e f) -> p u e f", e=2)
+            for half in range(2):
+                cols = slice(half * BANK, (half + 1) * BANK)
+                for u in range(2):
+                    nc.sync.dma_start(out=tile_view[:, u, :, cols], in_=view[:, u, :, cols])
 
-        def load_weights(c):
-            view = Wo_vid.rearrange("(c u p e) n -> p (c u) (e n)", c=F_PASSES, u=2, e=2)
-            nc.sync.dma_start(out=wo_raw[:, 2 * c : 2 * c + 2, :], in_=view[:, 2 * c : 2 * c + 2, :])
+        def load_weights(b):
+            view = Wo_vid.rearrange("(cu p e) n -> p cu e n", cu=2 * F_PASSES, e=2)
+            tile_view = wo_raw[:].rearrange("p cu (e n) -> p cu e n", e=2)
+            cols = slice(b * BANK, (b + 1) * BANK)
+            for cu in range(2 * F_PASSES):
+                nc.sync.dma_start(out=tile_view[:, cu, :, cols], in_=view[:, cu, :, cols])
 
         load_queries(0, [0])
         load_keys(0, range(NH // 2))
-        load_values(0)
-        load_keys(1, [0])
         load_queries(0, [1])
+        load_values(0)
         load_weights(0)
-        load_keys(1, [1])
-        load_weights(1)
         load_queries(0, [2])
-        nc.sync.dma_start(out=bias_bc[:], in_=bo_vid.partition_broadcast(P))
-        load_keys(1, [2])
+        load_weights(1)
+        load_keys(1, [0, 1])
         load_queries(0, [3])
-        load_keys(1, [3])
+        load_weights(2)
+        load_keys(1, [2, 3])
         load_values(1)
+        nc.sync.dma_start(out=bias_bc[:], in_=bo_vid.partition_broadcast(P))
         load_queries(1, range(Q_TILES))
 
         kT = [keep.tile([P, NH, WIN_LEN], BF16, name="kT%d" % n) for n in range(N_WIN)]
@@ -158,11 +164,13 @@ def tile_naswinattention_pb_kernel(tc, qw, kw, vw, Wo_vid, bo_vid, out):
                 out=kT[n][:, 2 * pair : 2 * pair + 2, :], in_=kT_ps[n, pair][:].rearrange("p h t k -> p h (t k)")
             )
 
-        def regroup(key, rows):
-            grouped[key] = work.tile([P, BANK, 4], BF16, name="grouped", tag="grouped_" + key[0], align_bytes=64)
+        def regroup(key, rows, piece):
+            if piece == 0:
+                grouped[key] = work.tile([P, BANK, 4], BF16, name="grouped", tag="grouped_" + key[0], align_bytes=64)
+            cols = slice(piece * (BANK // PIECES), (piece + 1) * (BANK // PIECES))
             nc.vector.tensor_copy(
-                out=grouped[key][:].rearrange("p (c i) t -> p c t i", i=4),
-                in_=rows.rearrange("p t (c i) -> p c t i", i=4),
+                out=grouped[key][:, cols, :].rearrange("p (c i) t -> p c t i", i=4),
+                in_=rows[:, :, cols].rearrange("p t (c i) -> p c t i", i=4),
             )
 
         def quantise_grouped(key, codes, scales):
@@ -183,6 +191,10 @@ def tile_naswinattention_pb_kernel(tc, qw, kw, vw, Wo_vid, bo_vid, out):
             nc.vector.tensor_reduce(
                 out=row_max[k][:, col : col + 1], in_=s_ps[i][:], axis=mybir.AxisListType.X, op=ALU.max
             )
+
+
+        def bias_of(i):
+            k, col = divmod(i, 4)
             nc.gpsimd.tensor_scalar(
                 out=exp_bias[k][:, col : col + 1],
                 in0=row_max[k][:, col : col + 1],
@@ -248,15 +260,16 @@ def tile_naswinattention_pb_kernel(tc, qw, kw, vw, Wo_vid, bo_vid, out):
             t, half = divmod(k, 2)
             if half == 0:
                 x_sb[t] = work.tile([P, INNER], BF16, name="x_sb", tag="x_sb")
+            if half in V_SCALES:
                 nc.vector.tensor_tensor(
-                    out=x_sb[t][:, : 4 * HD].rearrange("p (h d) -> p h d", h=4),
+                    out=x_sb[t][:, 4 * half * HD : 4 * (half + 1) * HD].rearrange("p (h d) -> p h d", h=4),
                     in0=o_ps[k][:],
                     in1=inv_sum[k][:].unsqueeze(2).to_broadcast([P, 4, HD]),
                     op=ALU.mult,
                 )
             else:
                 for h in range(4):
-                    d_cols = slice((4 + h) * HD, (4 + h + 1) * HD)
+                    d_cols = slice((4 * half + h) * HD, (4 * half + h + 1) * HD)
                     nc.scalar.activation(
                         out=x_sb[t][:, d_cols], in_=o_ps[k][:, h, :], func=ACT.Copy, scale=inv_sum[k][:, h : h + 1]
                     )
@@ -275,8 +288,8 @@ def tile_naswinattention_pb_kernel(tc, qw, kw, vw, Wo_vid, bo_vid, out):
             )
 
         def quantise_x(t):
-            x_codes[t] = work.tile([P, F_PASSES * P], U32, name="x_codes", tag="x_codes", align_bytes=64)
-            x_scales[t] = work.tile([P, F_PASSES * P], U8, name="x_scales", tag="x_scales", align_bytes=64)
+            x_codes[t] = keep.tile([P, F_PASSES * P], U32, name="x_codes%d" % t, align_bytes=64)
+            x_scales[t] = keep.tile([P, F_PASSES * P], U8, name="x_scales%d" % t, align_bytes=64)
             nc.vector.quantize_mx(out=x_codes[t][:].bitcast(FP8X4), scales=x_scales[t][:], in_=x_grouped[t][:])
 
         def project(t, b):
@@ -297,50 +310,80 @@ def tile_naswinattention_pb_kernel(tc, qw, kw, vw, Wo_vid, bo_vid, out):
         def add_bias_and_store(t, b):
             n, qt = divmod(t, Q_TILES)
             cols = slice(b * BANK, (b + 1) * BANK)
-            y_sb = work.tile([P, BANK], F32, name="y_sb", tag="y_sb", bufs=4)
+            y_sb = work.tile([P, BANK], F32, name="y_sb", tag="y_sb", bufs=8)
             nc.vector.tensor_tensor(out=y_sb[:], in0=y_ps[t, b][:], in1=bias_bc[:, cols], op=ALU.add)
             nc.sync.dma_start(out=out_rows[n, qt * 16 : (qt + 1) * 16, :, cols], in_=y_sb[:])
+
+        fillers = []
+
+        def prepare_v(n, first):
+            for half in range(2):
+                cols = slice(half * BANK, (half + 1) * BANK)
+                for piece in range(PIECES):
+                    fillers.append((first, regroup, (("v", n, half), v_rows[n][:, :, cols], piece)))
+                fillers.append((first, quantise_grouped, (("v", n, half), v_codes[n][:, cols], v_scales[n][:, cols])))
+
+        def prepare_wo():
+            for b in range(OUT_BANKS):
+                for c in range(F_PASSES):
+                    cols = slice(b * BANK, (b + 1) * BANK)
+                    for piece in range(PIECES):
+                        fillers.append((0, regroup, (("wo", c, b), wo_rows[:, c, :, cols], piece)))
+                    fillers.append((0, quantise_grouped, (("wo", c, b), wo_codes[:, c, cols], wo_scales[:, c, cols])))
+
+        prepare_v(0, V0_FIRST)
+        if V1_FIRST:
+            prepare_v(1, 0)
+            prepare_wo()
+        else:
+            prepare_wo()
+            prepare_v(1, 0)
+        for t in range(N_TILES):
+            for b in range(OUT_BANKS):
+                fillers.append((NH * t + NH - 1 + AT_QUANT_X + 2, add_bias_and_store, (t, b)))
+        at_step = {}
+        step = 0
+        for first, fn, args in fillers:
+            step = max(step, first)
+            while ends(step - AT_QUANT_E, 4) is not None:
+                step += 1
+            at_step[step] = (fn, args)
+            step += 1
+        LAST_STEP = step - 1
 
         for step in range(FIRST_STEP, LAST_STEP + 1):
             i = step - AT_TRANSPOSE_QK
             if starts(i, NH) is not None:
                 transpose_q(i // NH)
-            if starts(i, 2) is not None and i < NH:
-                transpose_k(0, i // 2)
             i = step - AT_COPY_QK
             if starts(i, NH) is not None:
                 copy_qT(i // NH)
+            i = step - AT_COPY_K
             if starts(i, 2) is not None and i < NH:
                 copy_kT(0, i // 2)
             tile_no, tile_step = divmod(step, NH)
-            if 0 <= tile_no < Q_TILES and tile_step == NEXT_K_STEP:
-                transpose_k(1, tile_no)
-            if 0 <= tile_no < Q_TILES and tile_step == NEXT_K_STEP + 1:
-                copy_kT(1, tile_no)
+            if step in NEXT_K_STEPS:
+                transpose_k(1, NEXT_K_STEPS.index(step))
+            if step - 1 in NEXT_K_STEPS:
+                copy_kT(1, NEXT_K_STEPS.index(step - 1))
 
             if 0 <= step - AT_SCORES < N_UNITS:
                 scores(step - AT_SCORES)
+            i = step - AT_TRANSPOSE_K
+            if starts(i, 2) is not None and i < NH:
+                transpose_k(0, i // 2)
             if 0 <= step - AT_MAX < N_UNITS:
                 maximum(step - AT_MAX)
             if 0 <= step - AT_EXP < N_UNITS:
                 exponential(step - AT_EXP)
+            if 0 <= step - AT_MAX < N_UNITS:
+                bias_of(step - AT_MAX)
 
-            for n in range(N_WIN):
-                if step in V_STEPS[n]:
-                    half, turn = divmod(V_STEPS[n].index(step), 2)
-                    cols = slice(half * BANK, (half + 1) * BANK)
-                    if turn == 0:
-                        regroup(("v", n, half), v_rows[n][:, :, cols])
-                    else:
-                        quantise_grouped(("v", n, half), v_codes[n][:, cols], v_scales[n][:, cols])
-            if WO_STEP <= step < WO_STEP + 2 * F_PASSES * OUT_BANKS:
-                chunk, turn = divmod(step - WO_STEP, 2)
-                c, b = divmod(chunk, OUT_BANKS)
-                cols = slice(b * BANK, (b + 1) * BANK)
-                if turn == 0:
-                    regroup(("wo", c, b), wo_rows[:, c, :, cols])
-                else:
-                    quantise_grouped(("wo", c, b), wo_codes[:, c, cols], wo_scales[:, c, cols])
+            if step in at_step:
+                fn, args = at_step[step]
+                fn(*args)
+            if step + 1 in at_step and at_step[step + 1][0] == add_bias_and_store:
+                project(*at_step[step + 1][1])
 
             j = ends(step - AT_FLIP_E, 2)
             if j is not None:
@@ -366,10 +409,3 @@ def tile_naswinattention_pb_kernel(tc, qw, kw, vw, Wo_vid, bo_vid, out):
             t = ends(step - AT_QUANT_X, NH)
             if t is not None:
                 quantise_x(t)
-            for b in range(OUT_BANKS):
-                t = ends(step - AT_PROJECT - b, NH)
-                if t is not None:
-                    project(t, b)
-                t = ends(step - AT_BIAS - b, NH)
-                if t is not None:
-                    add_bias_and_store(t, b)

@@ -50,6 +50,7 @@ NEXT_K_STEPS = (12, 18, 24, 30)
 V_SCALES = ()
 V1_FIRST = False
 V0_FIRST = 3
+S_BUFS = 4
 PIECES = 2
 
 
@@ -141,6 +142,7 @@ def tile_naswinattention_pb_kernel(tc, qw, kw, vw, Wo_vid, bo_vid, out):
         e_grouped, e_codes, e_scales, o_ps = {}, {}, {}, {}
         x_sb, xT_ps, x_grouped, x_codes, x_scales, y_ps = {}, {}, {}, {}, {}, {}
         grouped = {}
+        s_sb = {}
 
         def transpose_q(t):
             n, qt = divmod(t, Q_TILES)
@@ -186,23 +188,13 @@ def tile_naswinattention_pb_kernel(tc, qw, kw, vw, Wo_vid, bo_vid, out):
         def maximum(i):
             k, col = divmod(i, 4)
             if col == 0:
-                row_max[k] = work.tile([P, 4], F32, name="row_max", tag="row_max", bufs=4)
                 exp_bias[k] = work.tile([P, 4], F32, name="exp_bias", tag="exp_bias", bufs=4)
-            nc.vector.tensor_reduce(
-                out=row_max[k][:, col : col + 1], in_=s_ps[i][:], axis=mybir.AxisListType.X, op=ALU.max
+            s_sb[i] = work.tile([P, WIN_LEN], F32, name="s_sb", tag="s_sb", bufs=S_BUFS)
+            nc.vector.tensor_scalar(
+                out=s_sb[i][:], in0=s_ps[i][:], scalar1=-SCALE, scalar2=None, op0=ALU.mult, op1=ALU.min,
+                accum_out=exp_bias[k][:, col : col + 1],
             )
 
-
-        def bias_of(i):
-            k, col = divmod(i, 4)
-            nc.gpsimd.tensor_scalar(
-                out=exp_bias[k][:, col : col + 1],
-                in0=row_max[k][:, col : col + 1],
-                scalar1=-SCALE,
-                scalar2=0.0,
-                op0=ALU.mult,
-                op1=ALU.add,
-            )
 
         def exponential(i):
             k, col = divmod(i, 4)
@@ -211,10 +203,10 @@ def tile_naswinattention_pb_kernel(tc, qw, kw, vw, Wo_vid, bo_vid, out):
             e_sb[i] = work.tile([P, WIN_LEN], BF16, name="e_sb", tag="e_sb", bufs=8)
             nc.scalar.activation(
                 out=e_sb[i][:],
-                in_=s_ps[i][:],
+                in_=s_sb[i][:],
                 func=ACT.Exp,
                 bias=exp_bias[k][:, col : col + 1],
-                scale=SCALE,
+                scale=-1.0,
                 accum_out=row_sum[k][:, col : col + 1],
             )
 
@@ -376,8 +368,6 @@ def tile_naswinattention_pb_kernel(tc, qw, kw, vw, Wo_vid, bo_vid, out):
                 maximum(step - AT_MAX)
             if 0 <= step - AT_EXP < N_UNITS:
                 exponential(step - AT_EXP)
-            if 0 <= step - AT_MAX < N_UNITS:
-                bias_of(step - AT_MAX)
 
             if step in at_step:
                 fn, args = at_step[step]

@@ -45,7 +45,7 @@ AT_SCALE_O = 7
 AT_FLIP_X = 8
 AT_COPY_X = 9
 AT_QUANT_X = 10
-FIRST_STEP = AT_TRANSPOSE_QK
+FIRST_STEP = AT_TRANSPOSE_K
 NEXT_K_STEPS = (12, 18, 24, 30)
 V_SCALES = ()
 V1_FIRST = False
@@ -112,8 +112,13 @@ def tile_naswinattention_pb_kernel(tc, qw, kw, vw, Wo_vid, bo_vid, out):
             for cu in range(2 * F_PASSES):
                 nc.sync.dma_start(out=tile_view[:, cu, :, cols], in_=view[:, cu, :, cols])
 
-        load_queries(0, [0])
-        load_keys(0, range(NH // 2))
+        first = slice(0, 2 * HD)
+        rest = slice(2 * HD, INNER)
+        q_view = qw[0].rearrange("(t p) g d -> p t (g d)", p=P)
+        nc.sync.dma_start(out=q_raw[0][:, 0, first], in_=q_view[:, 0, first])
+        load_keys(0, [0])
+        nc.sync.dma_start(out=q_raw[0][:, 0, rest], in_=q_view[:, 0, rest])
+        load_keys(0, [1, 2, 3])
         load_queries(0, [1])
         load_values(0)
         load_weights(0)
@@ -127,7 +132,8 @@ def tile_naswinattention_pb_kernel(tc, qw, kw, vw, Wo_vid, bo_vid, out):
         nc.sync.dma_start(out=bias_bc[:], in_=bo_vid.partition_broadcast(P))
         load_queries(1, range(Q_TILES))
 
-        kT = [keep.tile([P, NH, WIN_LEN], BF16, name="kT%d" % n) for n in range(N_WIN)]
+        qk0 = keep.tile([P, NH, P + WIN_LEN], BF16, name="qk0")
+        kT1 = keep.tile([P, NH, WIN_LEN], BF16, name="kT1")
         v_codes = [keep.tile([P, INNER], U32, name="v_codes%d" % n, align_bytes=64) for n in range(N_WIN)]
         v_scales = [keep.tile([P, INNER], U8, name="v_scales%d" % n, align_bytes=64) for n in range(N_WIN)]
         wo_codes = keep.tile([P, F_PASSES, VID_DIM], U32, name="wo_codes", align_bytes=64)
@@ -142,6 +148,7 @@ def tile_naswinattention_pb_kernel(tc, qw, kw, vw, Wo_vid, bo_vid, out):
         e_grouped, e_codes, e_scales, o_ps = {}, {}, {}, {}
         x_sb, xT_ps, x_grouped, x_codes, x_scales, y_ps = {}, {}, {}, {}, {}, {}
         grouped = {}
+        qk_ps = {}
         s_sb = {}
 
         def transpose_q(t):
@@ -163,8 +170,18 @@ def tile_naswinattention_pb_kernel(tc, qw, kw, vw, Wo_vid, bo_vid, out):
 
         def copy_kT(n, pair):
             nc.scalar.copy(
-                out=kT[n][:, 2 * pair : 2 * pair + 2, :], in_=kT_ps[n, pair][:].rearrange("p h t k -> p h (t k)")
+                out=kT1[:, 2 * pair : 2 * pair + 2, :], in_=kT_ps[n, pair][:].rearrange("p h t k -> p h (t k)")
             )
+
+        def transpose_first(g):
+            cols = slice(g * HD, (g + 1) * HD)
+            qk_ps[g] = aux_banks.tile([P, 1 + Q_TILES, P], BF16, name="qk_ps", tag="aux")
+            nc.tensor.transpose(qk_ps[g][:, 0, :], q_raw[0][:, 0, cols], ident_bf[:])
+            for kt in range(Q_TILES):
+                nc.tensor.transpose(qk_ps[g][:, 1 + kt, :], k_raw[0][:, kt, cols], ident_bf[:])
+
+        def copy_first(g):
+            nc.scalar.copy(out=qk0[:, g, :], in_=qk_ps[g][:].rearrange("p a k -> p (a k)"))
 
         def regroup(key, rows, piece):
             if piece == 0:
@@ -183,7 +200,9 @@ def tile_naswinattention_pb_kernel(tc, qw, kw, vw, Wo_vid, bo_vid, out):
         def scores(i):
             t, g = divmod(i, NH)
             s_ps[i] = s_banks.tile([P, WIN_LEN], F32, name="s_ps", tag="s")
-            nc.tensor.matmul(s_ps[i][:], lhsT=qT[t][:, g, :], rhs=kT[t // Q_TILES][:, g, :], start=True, stop=True)
+            lhsT = qk0[:, g, :P] if t == 0 else qT[t][:, g, :]
+            rhs = qk0[:, g, P:] if t < Q_TILES else kT1[:, g, :]
+            nc.tensor.matmul(s_ps[i][:], lhsT=lhsT, rhs=rhs, start=True, stop=True)
 
         def maximum(i):
             k, col = divmod(i, 4)
@@ -345,14 +364,13 @@ def tile_naswinattention_pb_kernel(tc, qw, kw, vw, Wo_vid, bo_vid, out):
 
         for step in range(FIRST_STEP, LAST_STEP + 1):
             i = step - AT_TRANSPOSE_QK
-            if starts(i, NH) is not None:
+            if starts(i, NH) is not None and i > 0:
                 transpose_q(i // NH)
             i = step - AT_COPY_QK
-            if starts(i, NH) is not None:
+            if starts(i, NH) is not None and i > 0:
                 copy_qT(i // NH)
-            i = step - AT_COPY_K
-            if starts(i, 2) is not None and i < NH:
-                copy_kT(0, i // 2)
+            if 0 <= step - AT_COPY_K < NH:
+                copy_first(step - AT_COPY_K)
             tile_no, tile_step = divmod(step, NH)
             if step in NEXT_K_STEPS:
                 transpose_k(1, NEXT_K_STEPS.index(step))
@@ -361,9 +379,8 @@ def tile_naswinattention_pb_kernel(tc, qw, kw, vw, Wo_vid, bo_vid, out):
 
             if 0 <= step - AT_SCORES < N_UNITS:
                 scores(step - AT_SCORES)
-            i = step - AT_TRANSPOSE_K
-            if starts(i, 2) is not None and i < NH:
-                transpose_k(0, i // 2)
+            if 0 <= step - AT_TRANSPOSE_K < NH:
+                transpose_first(step - AT_TRANSPOSE_K)
             if 0 <= step - AT_MAX < N_UNITS:
                 maximum(step - AT_MAX)
             if 0 <= step - AT_EXP < N_UNITS:

@@ -44,11 +44,12 @@ AT_ATTEND = 6
 AT_SCALE_O = 7
 AT_FLIP_X = 8
 AT_COPY_X = 9
-AT_QUANT_X = 10
+AT_QUANT_X = 13
 FIRST_STEP = AT_TRANSPOSE_K
 NEXT_K_STEPS = (12, 18, 24, 30)
-V_SCALES = ()
-V1_FIRST = False
+V_SCALES = (0,)
+RING = 2
+PREP_FIRST = 8
 V0_FIRST = 3
 S_BUFS = 4
 PIECES = 2
@@ -183,14 +184,21 @@ def tile_naswinattention_pb_kernel(tc, qw, kw, vw, Wo_vid, bo_vid, out):
         def copy_first(g):
             nc.scalar.copy(out=qk0[:, g, :], in_=qk_ps[g][:].rearrange("p a k -> p (a k)"))
 
-        def regroup(key, rows, piece):
+        def regroup(key, rows, piece, engine):
             if piece == 0:
-                grouped[key] = work.tile([P, BANK, 4], BF16, name="grouped", tag="grouped_" + key[0], align_bytes=64)
+                grouped[key] = work.tile([P, BANK, 4], BF16, name="grouped", tag="grouped", bufs=RING, align_bytes=64)
             cols = slice(piece * (BANK // PIECES), (piece + 1) * (BANK // PIECES))
-            nc.vector.tensor_copy(
-                out=grouped[key][:, cols, :].rearrange("p (c i) t -> p c t i", i=4),
-                in_=rows[:, :, cols].rearrange("p t (c i) -> p c t i", i=4),
-            )
+            if engine == "vector":
+                nc.vector.tensor_copy(
+                    out=grouped[key][:, cols, :].rearrange("p (c i) t -> p c t i", i=4),
+                    in_=rows[:, :, cols].rearrange("p t (c i) -> p c t i", i=4),
+                )
+            else:
+                nc.gpsimd.tensor_scalar(
+                    out=grouped[key][:, cols, :],
+                    in0=rows[:, :, cols].rearrange("p t n -> p n t"),
+                    scalar1=1.0, scalar2=0.0, op0=ALU.mult, op1=ALU.add,
+                )
 
         def quantise_grouped(key, codes, scales):
             nc.vector.quantize_mx(
@@ -325,40 +333,31 @@ def tile_naswinattention_pb_kernel(tc, qw, kw, vw, Wo_vid, bo_vid, out):
             nc.vector.tensor_tensor(out=y_sb[:], in0=y_ps[t, b][:], in1=bias_bc[:, cols], op=ALU.add)
             nc.sync.dma_start(out=out_rows[n, qt * 16 : (qt + 1) * 16, :, cols], in_=y_sb[:])
 
-        fillers = []
+        prep = []
 
-        def prepare_v(n, first):
+        def prepare_v(n):
             for half in range(2):
                 cols = slice(half * BANK, (half + 1) * BANK)
-                for piece in range(PIECES):
-                    fillers.append((first, regroup, (("v", n, half), v_rows[n][:, :, cols], piece)))
-                fillers.append((first, quantise_grouped, (("v", n, half), v_codes[n][:, cols], v_scales[n][:, cols])))
+                prep.append((("v", n, half), v_rows[n][:, :, cols], v_codes[n][:, cols], v_scales[n][:, cols]))
 
-        def prepare_wo():
-            for b in range(OUT_BANKS):
-                for c in range(F_PASSES):
-                    cols = slice(b * BANK, (b + 1) * BANK)
-                    for piece in range(PIECES):
-                        fillers.append((0, regroup, (("wo", c, b), wo_rows[:, c, :, cols], piece)))
-                    fillers.append((0, quantise_grouped, (("wo", c, b), wo_codes[:, c, cols], wo_scales[:, c, cols])))
-
-        prepare_v(0, V0_FIRST)
-        if V1_FIRST:
-            prepare_v(1, 0)
-            prepare_wo()
-        else:
-            prepare_wo()
-            prepare_v(1, 0)
+        prepare_v(0)
+        for b in range(OUT_BANKS):
+            cols = slice(b * BANK, (b + 1) * BANK)
+            for c in range(F_PASSES):
+                prep.append((("wo", c, b), wo_rows[:, c, :, cols], wo_codes[:, c, cols], wo_scales[:, c, cols]))
+        prepare_v(1)
+        quant_at = [PREP_FIRST + 4 * j for j in range(len(prep))]
+        fillers = []
         for t in range(N_TILES):
             for b in range(OUT_BANKS):
-                fillers.append((NH * t + NH - 1 + AT_QUANT_X + 2, add_bias_and_store, (t, b)))
+                fillers.append((max(NH * t + NH - 1 + AT_QUANT_X + 2, quant_at[3 + 2 * b] + 2), t, b))
         at_step = {}
         step = 0
-        for first, fn, args in fillers:
+        for first, t, b in sorted(fillers):
             step = max(step, first)
-            while ends(step - AT_QUANT_E, 4) is not None:
+            while ends(step - AT_QUANT_E, 4) is not None or (ends(step - AT_SCALE_O, 4) is not None and ends(step - AT_SCALE_O, 4) % 2 in V_SCALES):
                 step += 1
-            at_step[step] = (fn, args)
+            at_step[step] = (add_bias_and_store, (t, b))
             step += 1
         LAST_STEP = step - 1
 
@@ -386,6 +385,9 @@ def tile_naswinattention_pb_kernel(tc, qw, kw, vw, Wo_vid, bo_vid, out):
             if 0 <= step - AT_EXP < N_UNITS:
                 exponential(step - AT_EXP)
 
+            if V0_FIRST <= step < V0_FIRST + 2 * PIECES:
+                half, piece = divmod(step - V0_FIRST, PIECES)
+                regroup(prep[half][0], prep[half][1], piece, "vector")
             if step in at_step:
                 fn, args = at_step[step]
                 fn(*args)
@@ -401,6 +403,15 @@ def tile_naswinattention_pb_kernel(tc, qw, kw, vw, Wo_vid, bo_vid, out):
             k = ends(step - AT_QUANT_E, 4)
             if k is not None:
                 quantise_e(k)
+            t = ends(step - AT_QUANT_X, NH)
+            if t is not None:
+                quantise_x(t)
+            for j in range(len(prep)):
+                if quant_at[j] == step:
+                    quantise_grouped(prep[j][0], prep[j][2], prep[j][3])
+                    if j + RING < len(prep):
+                        for piece in range(PIECES):
+                            regroup(prep[j + RING][0], prep[j + RING][1], piece, "gpsimd")
             k = ends(step - AT_ATTEND, 4)
             if k is not None:
                 attend(k)
@@ -413,6 +424,3 @@ def tile_naswinattention_pb_kernel(tc, qw, kw, vw, Wo_vid, bo_vid, out):
             t = ends(step - AT_COPY_X, NH)
             if t is not None:
                 copy_xT(t)
-            t = ends(step - AT_QUANT_X, NH)
-            if t is not None:
-                quantise_x(t)

@@ -355,7 +355,7 @@ def tile_naswinattention_pb_kernel(tc, qw, kw, vw, Wo_vid, bo_vid, out):
         step = 0
         for first, t, b in sorted(fillers):
             step = max(step, first)
-            while ends(step - AT_QUANT_E, 4) is not None or (ends(step - AT_SCALE_O, 4) is not None and ends(step - AT_SCALE_O, 4) % 2 in V_SCALES):
+            while step < N_UNITS and step % NH not in (6, 7):
                 step += 1
             at_step[step] = (add_bias_and_store, (t, b))
             step += 1

@@ -37,22 +37,33 @@ AT_COPY_K = -2
 AT_SCORES = -1
 AT_MAX = 0
 AT_EXP = 1
-AT_FLIP_E = 3
-AT_COPY_E = 4
-AT_QUANT_E = 5
-AT_ATTEND = 6
-AT_SCALE_O = 7
-AT_FLIP_X = 8
-AT_COPY_X = 9
-AT_QUANT_X = 13
+AT_FLIP_E = 2
+AT_COPY_E = 3
+AT_QUANT_E = 4
+AT_ATTEND = 5
+AT_SCALE_O = 6
+AT_FLIP_X = 7
+AT_COPY_X = 8
+AT_QUANT_X = 12
 FIRST_STEP = AT_TRANSPOSE_K
 NEXT_K_STEPS = (12, 18, 24, 30)
 V_SCALES = (0,)
 RING = 2
-PREP_FIRST = 8
+EARLY_X = 7
+PREP_FIRST = 7
 V0_FIRST = 3
 S_BUFS = 4
 PIECES = 2
+
+
+def x_ready(step):
+    t = ends(step - AT_QUANT_X, NH)
+    if t is not None and t < EARLY_X:
+        return t
+    t = ends(step - AT_COPY_X - 1, NH)
+    if t is not None and t >= EARLY_X:
+        return t
+    return None
 
 
 def starts(i, size):
@@ -350,12 +361,12 @@ def tile_naswinattention_pb_kernel(tc, qw, kw, vw, Wo_vid, bo_vid, out):
         fillers = []
         for t in range(N_TILES):
             for b in range(OUT_BANKS):
-                fillers.append((max(NH * t + NH - 1 + AT_QUANT_X + 2, quant_at[3 + 2 * b] + 2), t, b))
+                fillers.append((max(NH * t + NH - 1 + (AT_QUANT_X if t < EARLY_X else AT_COPY_X + 1) + 2, quant_at[3 + 2 * b] + 2), t, b))
         at_step = {}
         step = 0
         for first, t, b in sorted(fillers):
             step = max(step, first)
-            while step < N_UNITS and step % NH not in (6, 7):
+            while step < N_UNITS and step % NH not in ((5, 6) if step > quant_at[-1] else (6,)):
                 step += 1
             at_step[step] = (add_bias_and_store, (t, b))
             step += 1
@@ -403,7 +414,7 @@ def tile_naswinattention_pb_kernel(tc, qw, kw, vw, Wo_vid, bo_vid, out):
             k = ends(step - AT_QUANT_E, 4)
             if k is not None:
                 quantise_e(k)
-            t = ends(step - AT_QUANT_X, NH)
+            t = x_ready(step)
             if t is not None:
                 quantise_x(t)
             for j in range(len(prep)):

@@ -366,7 +366,7 @@ def tile_naswinattention_pb_kernel(tc, qw, kw, vw, Wo_vid, bo_vid, out):
         step = 0
         for first, t, b in sorted(fillers):
             step = max(step, first)
-            while step < N_UNITS and step % NH not in ((5, 6) if step > quant_at[-1] else (6,)):
+            while step < N_UNITS and step % NH not in (5, 6):
                 step += 1
             at_step[step] = (add_bias_and_store, (t, b))
             step += 1

from contextlib import ExitStack

import concourse.mybir as mybir
from concourse.masks import make_identity

BF16 = mybir.dt.bfloat16
F32 = mybir.dt.float32
U32 = mybir.dt.uint32
U8 = mybir.dt.uint8
FP8X4 = mybir.dt.float8_e4m3fn_x4
ALU = mybir.AluOpType
ACT = mybir.ActivationFunctionType

P = 128
N_WIN = 2
WIN_LEN = 512
NH = 8
HD = 128
INNER = NH * HD
VID_DIM = 1536
Q_TILES = WIN_LEN // P
N_TILES = N_WIN * Q_TILES
N_UNITS = N_TILES * NH
WIN_UNITS = Q_TILES * NH
K_PASS = 512
F_PASSES = INNER // K_PASS
BANK = 512
OUT_BANKS = VID_DIM // BANK
SCALE = 1.0 / (HD ** 0.5)

FLOPS = 2 * 2 * N_WIN * NH * WIN_LEN * WIN_LEN * HD + 2 * N_WIN * WIN_LEN * INNER * VID_DIM

AT_TRANSPOSE_QK = -5
AT_COPY_QK = -4
AT_TRANSPOSE_K = -3
AT_COPY_K = -2
AT_SCORES = -1
AT_MAX = 0
AT_EXP = 1
AT_FLIP_E = 2
AT_COPY_E = 3
AT_QUANT_E = 4
AT_ATTEND = 5
AT_SCALE_O = 6
AT_FLIP_X = 7
AT_COPY_X = 8
AT_QUANT_X = 12
FIRST_STEP = AT_TRANSPOSE_K
NEXT_K_STEPS = (12, 18, 24, 30)
V_SCALES = (0,)
RING = 2
EARLY_X = 7
PREP_FIRST = 7
V0_FIRST = 3
S_BUFS = 4
PIECES = 2


def x_ready(step):
    t = ends(step - AT_QUANT_X, NH)
    if t is not None and t < EARLY_X:
        return t
    t = ends(step - AT_COPY_X - 1, NH)
    if t is not None and t >= EARLY_X:
        return t
    return None


def starts(i, size):
    if 0 <= i < N_UNITS and i % size == 0:
        return i // size
    return None


def ends(i, size):
    if 0 <= i < N_UNITS and i % size == size - 1:
        return i // size
    return None


def tile_naswinattention_pb_kernel(tc, qw, kw, vw, Wo_vid, bo_vid, out):
    nc = tc.nc
    with ExitStack() as ctx:
        keep = ctx.enter_context(tc.tile_pool(name="keep", bufs=1))
        work = ctx.enter_context(tc.tile_pool(name="work", bufs=2))
        s_banks = ctx.enter_context(tc.psum_pool(name="s_banks", bufs=3))
        aux_banks = ctx.enter_context(tc.psum_pool(name="aux_banks", bufs=5))
        ctx.enter_context(tc.manual_schedule())

        ident_bf = keep.tile([P, P], BF16, name="ident_bf")
        make_identity(nc, ident_bf[:])
        ident_f32 = keep.tile([P, P], F32, name="ident_f32")
        make_identity(nc, ident_f32[:])

        q_raw = [keep.tile([P, Q_TILES, INNER], BF16, name="q_raw%d" % n) for n in range(N_WIN)]
        k_raw = [keep.tile([P, Q_TILES, INNER], BF16, name="k_raw%d" % n) for n in range(N_WIN)]
        v_raw = [keep.tile([P, 2, 2 * INNER], BF16, name="v_raw%d" % n) for n in range(N_WIN)]
        wo_raw = keep.tile([P, 2 * F_PASSES, 2 * VID_DIM], BF16, name="wo_raw")
        bias_bc = keep.tile([P, VID_DIM], BF16, name="bias_bc")

        def load_queries(n, tiles):
            view = qw[n].rearrange("(t p) g d -> p t (g d)", p=P)
            for t in tiles:
                nc.sync.dma_start(out=q_raw[n][:, t, :], in_=view[:, t, :])

        def load_keys(n, pairs):
            view = kw[n].rearrange("(t p) g d -> p t (g d)", p=P)
            for pair in pairs:
                cols = slice(2 * pair * HD, (2 * pair + 2) * HD)
                nc.sync.dma_start(out=k_raw[n][:, :, cols], in_=view[:, :, cols])

        def load_values(n):
            view = vw[n].rearrange("(u p e) g d -> p u e (g d)", u=2, e=2)
            tile_view = v_raw[n][:].rearrange("p u (e f) -> p u e f", e=2)
            for half in range(2):
                cols = slice(half * BANK, (half + 1) * BANK)
                for u in range(2):
                    nc.sync.dma_start(out=tile_view[:, u, :, cols], in_=view[:, u, :, cols])

        def load_weights(b):
            view = Wo_vid.rearrange("(cu p e) n -> p cu e n", cu=2 * F_PASSES, e=2)
            tile_view = wo_raw[:].rearrange("p cu (e n) -> p cu e n", e=2)
            cols = slice(b * BANK, (b + 1) * BANK)
            for cu in range(2 * F_PASSES):
                nc.sync.dma_start(out=tile_view[:, cu, :, cols], in_=view[:, cu, :, cols])

        first = slice(0, 2 * HD)
        rest = slice(2 * HD, INNER)
        q_view = qw[0].rearrange("(t p) g d -> p t (g d)", p=P)
        nc.sync.dma_start(out=q_raw[0][:, 0, first], in_=q_view[:, 0, first])
        load_keys(0, [0])
        nc.sync.dma_start(out=q_raw[0][:, 0, rest], in_=q_view[:, 0, rest])
        load_keys(0, [1, 2, 3])
        load_queries(0, [1])
        load_values(0)
        load_weights(0)
        load_queries(0, [2])
        load_weights(1)
        load_keys(1, [0, 1])
        load_queries(0, [3])
        load_weights(2)
        load_keys(1, [2, 3])
        load_values(1)
        nc.sync.dma_start(out=bias_bc[:], in_=bo_vid.partition_broadcast(P))
        load_queries(1, range(Q_TILES))

        qk0 = keep.tile([P, NH, P + WIN_LEN], BF16, name="qk0")
        kT1 = keep.tile([P, NH, WIN_LEN], BF16, name="kT1")
        v_codes = [keep.tile([P, INNER], U32, name="v_codes%d" % n, align_bytes=64) for n in range(N_WIN)]
        v_scales = [keep.tile([P, INNER], U8, name="v_scales%d" % n, align_bytes=64) for n in range(N_WIN)]
        wo_codes = keep.tile([P, F_PASSES, VID_DIM], U32, name="wo_codes", align_bytes=64)
        wo_scales = keep.tile([P, F_PASSES, VID_DIM], U8, name="wo_scales", align_bytes=64)

        v_rows = [v_raw[n][:].rearrange("p u (e f) -> p (u e) f", e=2) for n in range(N_WIN)]
        wo_rows = wo_raw[:].rearrange("p (c u) (e n) -> p c (u e) n", u=2, e=2)
        out_rows = out.rearrange("(th n w) c -> n th w c", n=N_WIN, w=8)

        qT_ps, qT, kT_ps, s_ps, e_sb, eT_ps = {}, {}, {}, {}, {}, {}
        row_max, exp_bias, row_sum, inv_sum = {}, {}, {}, {}
        e_grouped, e_codes, e_scales, o_ps = {}, {}, {}, {}
        x_sb, xT_ps, x_grouped, x_codes, x_scales, y_ps = {}, {}, {}, {}, {}, {}
        grouped = {}
        qk_ps = {}
        s_sb = {}

        def transpose_q(t):
            n, qt = divmod(t, Q_TILES)
            qT_ps[t] = aux_banks.tile([P, NH, P], BF16, name="qT_ps", tag="aux")
            for g in range(NH):
                nc.tensor.transpose(qT_ps[t][:, g, :], q_raw[n][:, qt, g * HD : (g + 1) * HD], ident_bf[:])

        def copy_qT(t):
            qT[t] = work.tile([P, NH, P], BF16, name="qT", tag="qT")
            nc.scalar.copy(out=qT[t][:], in_=qT_ps[t][:])

        def transpose_k(n, pair):
            kT_ps[n, pair] = aux_banks.tile([P, 2, Q_TILES, P], BF16, name="kT_ps", tag="aux")
            for h in range(2):
                g = 2 * pair + h
                for kt in range(Q_TILES):
                    nc.tensor.transpose(kT_ps[n, pair][:, h, kt, :], k_raw[n][:, kt, g * HD : (g + 1) * HD], ident_bf[:])

        def copy_kT(n, pair):
            nc.scalar.copy(
                out=kT1[:, 2 * pair : 2 * pair + 2, :], in_=kT_ps[n, pair][:].rearrange("p h t k -> p h (t k)")
            )

        def transpose_first(g):
            cols = slice(g * HD, (g + 1) * HD)
            qk_ps[g] = aux_banks.tile([P, 1 + Q_TILES, P], BF16, name="qk_ps", tag="aux")
            nc.tensor.transpose(qk_ps[g][:, 0, :], q_raw[0][:, 0, cols], ident_bf[:])
            for kt in range(Q_TILES):
                nc.tensor.transpose(qk_ps[g][:, 1 + kt, :], k_raw[0][:, kt, cols], ident_bf[:])

        def copy_first(g):
            nc.scalar.copy(out=qk0[:, g, :], in_=qk_ps[g][:].rearrange("p a k -> p (a k)"))

        def regroup(key, rows, piece, engine):
            if piece == 0:
                grouped[key] = work.tile([P, BANK, 4], BF16, name="grouped", tag="grouped", bufs=RING, align_bytes=64)
            cols = slice(piece * (BANK // PIECES), (piece + 1) * (BANK // PIECES))
            if engine == "vector":
                nc.vector.tensor_copy(
                    out=grouped[key][:, cols, :].rearrange("p (c i) t -> p c t i", i=4),
                    in_=rows[:, :, cols].rearrange("p t (c i) -> p c t i", i=4),
                )
            else:
                nc.gpsimd.tensor_scalar(
                    out=grouped[key][:, cols, :],
                    in0=rows[:, :, cols].rearrange("p t n -> p n t"),
                    scalar1=1.0, scalar2=0.0, op0=ALU.mult, op1=ALU.add,
                )

        def quantise_grouped(key, codes, scales):
            nc.vector.quantize_mx(
                out=codes.bitcast(FP8X4), scales=scales, in_=grouped[key][:].rearrange("p f t -> p (f t)")
            )

        def scores(i):
            t, g = divmod(i, NH)
            s_ps[i] = s_banks.tile([P, WIN_LEN], F32, name="s_ps", tag="s")
            lhsT = qk0[:, g, :P] if t == 0 else qT[t][:, g, :]
            rhs = qk0[:, g, P:] if t < Q_TILES else kT1[:, g, :]
            nc.tensor.matmul(s_ps[i][:], lhsT=lhsT, rhs=rhs, start=True, stop=True)

        def maximum(i):
            k, col = divmod(i, 4)
            if col == 0:
                exp_bias[k] = work.tile([P, 4], F32, name="exp_bias", tag="exp_bias", bufs=4)
            s_sb[i] = work.tile([P, WIN_LEN], F32, name="s_sb", tag="s_sb", bufs=S_BUFS)
            nc.vector.tensor_scalar(
                out=s_sb[i][:], in0=s_ps[i][:], scalar1=-SCALE, scalar2=None, op0=ALU.mult, op1=ALU.min,
                accum_out=exp_bias[k][:, col : col + 1],
            )


        def exponential(i):
            k, col = divmod(i, 4)
            if col == 0:
                row_sum[k] = work.tile([P, 4], F32, name="row_sum", tag="row_sum", bufs=4)
            e_sb[i] = work.tile([P, WIN_LEN], BF16, name="e_sb", tag="e_sb", bufs=8)
            nc.scalar.activation(
                out=e_sb[i][:],
                in_=s_sb[i][:],
                func=ACT.Exp,
                bias=exp_bias[k][:, col : col + 1],
                scale=-1.0,
                accum_out=row_sum[k][:, col : col + 1],
            )

        def flip_e(j):
            eT_ps[j] = aux_banks.tile([P, 2, 2, P], F32, name="eT_ps", tag="aux")
            for h in range(2):
                words = e_sb[2 * j + h][:].bitcast(F32)
                for u in range(2):
                    nc.tensor.transpose(eT_ps[j][:, h, u, :], words[:, u * P : (u + 1) * P], ident_f32[:])

        def copy_eT(j):
            k, half = divmod(j, 2)
            if half == 0:
                e_grouped[k] = work.tile([P, 4 * WIN_LEN], BF16, name="e_grouped", tag="e_grouped", bufs=3, align_bytes=64)
            dst = e_grouped[k][:].bitcast(F32).rearrange("p (h q u) -> p h q u", h=4, u=2)
            nc.scalar.copy(out=dst[:, 2 * half : 2 * half + 2, :, :], in_=eT_ps[j][:].rearrange("p h u q -> p h q u"))

        def quantise_e(k):
            inv_sum[k] = work.tile([P, 4], F32, name="inv_sum", tag="inv_sum", bufs=3)
            nc.vector.reciprocal(out=inv_sum[k][:], in_=row_sum[k][:])
            e_codes[k] = work.tile([P, WIN_LEN], U32, name="e_codes", tag="e_codes", align_bytes=64)
            e_scales[k] = work.tile([P, WIN_LEN], U8, name="e_scales", tag="e_scales", align_bytes=64)
            nc.vector.quantize_mx(out=e_codes[k][:].bitcast(FP8X4), scales=e_scales[k][:], in_=e_grouped[k][:])

        def attend(k):
            t, half = divmod(k, 2)
            n = t // Q_TILES
            o_ps[k] = aux_banks.tile([P, 4, HD], F32, name="o_ps", tag="aux")
            for h in range(4):
                q_cols = slice(h * P, (h + 1) * P)
                d_cols = slice((4 * half + h) * HD, (4 * half + h + 1) * HD)
                nc.tensor.matmul_mx(
                    out=o_ps[k][:, h, :],
                    lhsT=e_codes[k][:, q_cols].bitcast(FP8X4),
                    lhsT_scale=e_scales[k][:, q_cols],
                    rhs=v_codes[n][:, d_cols].bitcast(FP8X4),
                    rhs_scale=v_scales[n][:, d_cols],
                    start=True,
                    stop=True,
                )

        def scale_o(k):
            t, half = divmod(k, 2)
            if half == 0:
                x_sb[t] = work.tile([P, INNER], BF16, name="x_sb", tag="x_sb")
            if half in V_SCALES:
                nc.vector.tensor_tensor(
                    out=x_sb[t][:, 4 * half * HD : 4 * (half + 1) * HD].rearrange("p (h d) -> p h d", h=4),
                    in0=o_ps[k][:],
                    in1=inv_sum[k][:].unsqueeze(2).to_broadcast([P, 4, HD]),
                    op=ALU.mult,
                )
            else:
                for h in range(4):
                    d_cols = slice((4 * half + h) * HD, (4 * half + h + 1) * HD)
                    nc.scalar.activation(
                        out=x_sb[t][:, d_cols], in_=o_ps[k][:, h, :], func=ACT.Copy, scale=inv_sum[k][:, h : h + 1]
                    )

        def flip_x(t):
            xT_ps[t] = aux_banks.tile([P, 2 * F_PASSES, P], F32, name="xT_ps", tag="aux")
            words = x_sb[t][:].bitcast(F32)
            for cu in range(2 * F_PASSES):
                nc.tensor.transpose(xT_ps[t][:, cu, :], words[:, cu * P : (cu + 1) * P], ident_f32[:])

        def copy_xT(t):
            x_grouped[t] = work.tile([P, F_PASSES * P * 4], BF16, name="x_grouped", tag="x_grouped", align_bytes=64)
            nc.scalar.copy(
                out=x_grouped[t][:].bitcast(F32).rearrange("p (c q u) -> p c q u", c=F_PASSES, u=2),
                in_=xT_ps[t][:].rearrange("p (c u) q -> p c q u", u=2),
            )

        def quantise_x(t):
            x_codes[t] = keep.tile([P, F_PASSES * P], U32, name="x_codes%d" % t, align_bytes=64)
            x_scales[t] = keep.tile([P, F_PASSES * P], U8, name="x_scales%d" % t, align_bytes=64)
            nc.vector.quantize_mx(out=x_codes[t][:].bitcast(FP8X4), scales=x_scales[t][:], in_=x_grouped[t][:])

        def project(t, b):
            cols = slice(b * BANK, (b + 1) * BANK)
            y_ps[t, b] = aux_banks.tile([P, BANK], F32, name="y_ps", tag="aux")
            for c in range(F_PASSES):
                toks = slice(c * P, (c + 1) * P)
                nc.tensor.matmul_mx(
                    out=y_ps[t, b][:],
                    lhsT=x_codes[t][:, toks].bitcast(FP8X4),
                    lhsT_scale=x_scales[t][:, toks],
                    rhs=wo_codes[:, c, cols].bitcast(FP8X4),
                    rhs_scale=wo_scales[:, c, cols],
                    start=(c == 0),
                    stop=(c == F_PASSES - 1),
                )

        def add_bias_and_store(t, b):
            n, qt = divmod(t, Q_TILES)
            cols = slice(b * BANK, (b + 1) * BANK)
            y_sb = work.tile([P, BANK], F32, name="y_sb", tag="y_sb", bufs=8)
            nc.vector.tensor_tensor(out=y_sb[:], in0=y_ps[t, b][:], in1=bias_bc[:, cols], op=ALU.add)
            nc.sync.dma_start(out=out_rows[n, qt * 16 : (qt + 1) * 16, :, cols], in_=y_sb[:])

        prep = []

        def prepare_v(n):
            for half in range(2):
                cols = slice(half * BANK, (half + 1) * BANK)
                prep.append((("v", n, half), v_rows[n][:, :, cols], v_codes[n][:, cols], v_scales[n][:, cols]))

        prepare_v(0)
        for b in range(OUT_BANKS):
            cols = slice(b * BANK, (b + 1) * BANK)
            for c in range(F_PASSES):
                prep.append((("wo", c, b), wo_rows[:, c, :, cols], wo_codes[:, c, cols], wo_scales[:, c, cols]))
        prepare_v(1)
        quant_at = [PREP_FIRST + 4 * j for j in range(len(prep))]
        fillers = []
        for t in range(N_TILES):
            for b in range(OUT_BANKS):
                fillers.append((max(NH * t + NH - 1 + (AT_QUANT_X if t < EARLY_X else AT_COPY_X + 1) + 2, quant_at[3 + 2 * b] + 2), t, b))
        at_step = {}
        step = 0
        for first, t, b in sorted(fillers):
            step = max(step, first)
            while step < N_UNITS and step % NH not in (5, 6):
                step += 1
            at_step[step] = (add_bias_and_store, (t, b))
            step += 1
        LAST_STEP = step - 1

        for step in range(FIRST_STEP, LAST_STEP + 1):
            i = step - AT_TRANSPOSE_QK
            if starts(i, NH) is not None and i > 0:
                transpose_q(i // NH)
            i = step - AT_COPY_QK
            if starts(i, NH) is not None and i > 0:
                copy_qT(i // NH)
            if 0 <= step - AT_COPY_K < NH:
                copy_first(step - AT_COPY_K)
            tile_no, tile_step = divmod(step, NH)
            if step in NEXT_K_STEPS:
                transpose_k(1, NEXT_K_STEPS.index(step))
            if step - 1 in NEXT_K_STEPS:
                copy_kT(1, NEXT_K_STEPS.index(step - 1))

            if 0 <= step - AT_SCORES < N_UNITS:
                scores(step - AT_SCORES)
            if 0 <= step - AT_TRANSPOSE_K < NH:
                transpose_first(step - AT_TRANSPOSE_K)
            if 0 <= step - AT_MAX < N_UNITS:
                maximum(step - AT_MAX)
            if 0 <= step - AT_EXP < N_UNITS:
                exponential(step - AT_EXP)

            if V0_FIRST <= step < V0_FIRST + 2 * PIECES:
                half, piece = divmod(step - V0_FIRST, PIECES)
                regroup(prep[half][0], prep[half][1], piece, "vector")
            if step in at_step:
                fn, args = at_step[step]
                fn(*args)
            if step + 1 in at_step and at_step[step + 1][0] == add_bias_and_store:
                project(*at_step[step + 1][1])

            j = ends(step - AT_FLIP_E, 2)
            if j is not None:
                flip_e(j)
            j = ends(step - AT_COPY_E, 2)
            if j is not None:
                copy_eT(j)
            k = ends(step - AT_QUANT_E, 4)
            if k is not None:
                quantise_e(k)
            t = x_ready(step)
            if t is not None:
                quantise_x(t)
            for j in range(len(prep)):
                if quant_at[j] == step:
                    quantise_grouped(prep[j][0], prep[j][2], prep[j][3])
                    if j + RING < len(prep):
                        for piece in range(PIECES):
                            regroup(prep[j + RING][0], prep[j + RING][1], piece, "gpsimd")
            k = ends(step - AT_ATTEND, 4)
            if k is not None:
                attend(k)
            k = ends(step - AT_SCALE_O, 4)
            if k is not None:
                scale_o(k)
            t = ends(step - AT_FLIP_X, NH)
            if t is not None:
                flip_x(t)
            t = ends(step - AT_COPY_X, NH)
            if t is not None:
                copy_xT(t)
